import numpy as np
import ml_dtypes


def mxq(x, axis, fmt="e4m3"):
    dtype, down = {"e4m3": (ml_dtypes.float8_e4m3fn, 7), "e5m2": (ml_dtypes.float8_e5m2, 14)}[fmt]
    v = np.moveaxis(np.asarray(x, np.float32).astype(ml_dtypes.bfloat16).astype(np.float64), axis, -1)
    blocks = v.reshape(v.shape[:-1] + (-1, 32))
    amax = np.abs(blocks).max(-1, keepdims=True)
    byte = np.maximum(np.where(amax > 0, np.frexp(amax)[1] - 1 + 127, 0) - down, 1)
    scale = np.exp2(byte - 127.0)
    codes = (blocks / scale).astype(np.float32).astype(dtype).astype(np.float64)
    return np.moveaxis((codes * scale).reshape(v.shape), -1, axis)


WIDE = False


def mx_kscale(k):
    if not WIDE:
        return np.ones(k)
    levels = np.array([30, -30])
    if k % 512:
        return np.exp2(np.random.permutation(np.resize(levels, k // 32))).repeat(32)
    a = np.empty((k // 512, 16))
    for p in range(k // 512):
        a[p, :8] = np.random.permutation(np.resize(levels, 8))
        for g in range(8):
            far = levels[np.abs(levels - a[p, g]) >= 10]
            a[p, g + 8] = far[np.random.randint(len(far))]
    return np.exp2(a.ravel()).repeat(32)


BF16 = ml_dtypes.bfloat16


def bf(x):
    return np.asarray(x, np.float32).astype(BF16)


def f64(x):
    return np.asarray(x).astype(np.float64)


B, I, H = 4096, 256, 512


def sigmoid(v):
    return 1.0 / (1.0 + np.exp(-v))


def setup_inputs():
    s = mx_kscale(H)
    return {"x_t": bf(np.random.standard_normal((B, I))),
            "h": bf(np.random.standard_normal((B, H)) * s),
            "c": bf(np.random.standard_normal((B, H))),
            "W_ih": bf(np.random.standard_normal((4 * H, I)) * 0.7 / np.sqrt(I)),
            "W_hh": bf(np.random.standard_normal((4 * H, H)) * 0.7 / np.sqrt(H) / s),
            "b_ih": bf(np.random.standard_normal(4 * H) * 0.3),
            "b_hh": bf(np.random.standard_normal(4 * H) * 0.3)}


def reference(x_t, h, c, W_ih, W_hh, b_ih, b_hh):
    gates = f64(x_t) @ f64(W_ih).T + f64(b_ih) + (mxq(f64(h), 1, "e5m2") @ mxq(f64(W_hh), 1, "e5m2").T) + f64(b_hh)
    i, f, g, o = np.split(gates, 4, axis=1)
    c_next = sigmoid(f) * f64(c) + sigmoid(i) * np.tanh(g)
    h_next = sigmoid(o) * np.tanh(c_next)
    return h_next, c_next

@@ -1,0 +1,348 @@
+from contextlib import ExitStack
+
+import concourse.mybir as mybir
+from concourse.masks import make_identity
+
+B, I, H = 4096, 256, 512
+FLOPS = 2 * B * 4 * H * (I + H)
+
+F32 = mybir.dt.float32
+BF16 = mybir.dt.bfloat16
+I32 = mybir.dt.int32
+U32 = mybir.dt.uint32
+U8 = mybir.dt.uint8
+E5M2X4 = mybir.dt.float8_e5m2_x4
+ACT = mybir.ActivationFunctionType
+ALU = mybir.AluOpType
+
+P = 128
+TILES = B // P
+CHUNK = 4
+CHUNKS = TILES // CHUNK
+GATE_BLOCK = {"i": 0, "f": 1, "g": 2, "o": 3}
+AHEAD = 5
+RAMP = 3
+LAG = 4
+VECTOR_FROM = 30
+
+
+def tile_nodelstmcell_pa_t_kernel(tc, x_t, h, c, W_ih, W_hh, b_ih, b_hh, out_0, out_1):
+    nc = tc.nc
+    x_rows = x_t.rearrange("(q p j) k -> q p j k", p=P, j=CHUNK)
+    h_rows = h.rearrange("(q p j) k -> q p j k", p=P, j=CHUNK)
+    c_rows = c.rearrange("(q p j) k -> q p j k", p=P, j=CHUNK)
+    h_out = out_0.rearrange("(q p j) k -> q j p k", p=P, j=CHUNK)
+    c_out = out_1.rearrange("(q p j) k -> q j p k", p=P, j=CHUNK)
+    wih_rows = W_ih.rearrange("(g j p) k -> g p j k", p=P, j=4)
+    whh_rows = W_hh.rearrange("(g j p) k -> g p j k", p=P, j=4)
+
+    with ExitStack() as ctx:
+        keep = ctx.enter_context(tc.tile_pool(name="keep", bufs=1))
+        work = ctx.enter_context(tc.tile_pool(name="work", bufs=2))
+        psum = ctx.enter_context(tc.psum_pool(name="psum", bufs=1))
+        ctx.enter_context(tc.manual_schedule())
+
+        ident_bf = keep.tile([P, P], BF16, name="ident_bf")
+        ident_f32 = keep.tile([P, P], F32, name="ident_f32")
+        ones = keep.tile([P, P], BF16, name="ones")
+        bias_rows = keep.tile([P, 4 * H], BF16, name="bias_rows")
+        bias_bc = {g: keep.tile([P, H], F32, name="bias_bc_" + g) for g in "fio"}
+        wih_t = {g: keep.tile([P, 2, H], BF16, name="wih_t_" + g) for g in "figo"}
+        whh_codes = {g: keep.tile([P, H], U32, name="whh_codes_" + g, align_bytes=64) for g in "figo"}
+        whh_scales = {g: keep.tile([P, H], U8, name="whh_scales_" + g, align_bytes=64) for g in "figo"}
+        x_sb = [keep.tile([P, CHUNK, I], BF16, name="x_sb%d" % q) for q in range(CHUNKS)]
+        h_sb = [keep.tile([P, CHUNK, H], BF16, name="h_sb%d" % q) for q in range(CHUNKS)]
+
+        wih_raw, whh_raw, c_sb = {}, {}, {}
+        x_tr, h_words, h_codes, h_scales, turn_bank = {}, {}, {}, {}, {}
+        z_fi, z_o, z_g, s_fi, s_o, t_g, c_new, t_c = {}, {}, {}, {}, {}, {}, {}, {}
+
+        def bank(tag, bufs, dtype=F32, width=H):
+            return psum.tile([P, width], dtype, name=tag, tag=tag, bufs=bufs)
+
+        def turn_tile():
+            return bank("turn", 2)
+
+        def mx_bank():
+            return bank("mx", 3)
+
+        def words_tile():
+            return work.tile([P, 4 * H], BF16, name="words", tag="words", bufs=3, align_bytes=64)
+
+        def fi_sized(dtype, shape):
+            return work.tile(shape, dtype, name="s_fi", tag="s_fi", bufs=LAG + 1)
+
+        def o_sized(dtype, shape):
+            return work.tile(shape, dtype, name="s_o", tag="s_o", bufs=2 * LAG)
+
+        def load_wih(g):
+            wih_raw[g] = o_sized(BF16, [P, 4, I])
+            nc.sync.dma_start(out=wih_raw[g][:], in_=wih_rows[GATE_BLOCK[g]])
+
+        def load_whh(g):
+            whh_raw[g] = fi_sized(BF16, [P, 4, H])
+            nc.sync.dma_start(out=whh_raw[g][:], in_=whh_rows[GATE_BLOCK[g]])
+
+        def load_x(q, js=slice(0, CHUNK)):
+            nc.sync.dma_start(out=x_sb[q][:, js, :], in_=x_rows[q][:, js, :])
+
+        def load_h(q, js=slice(0, CHUNK)):
+            nc.sync.dma_start(out=h_sb[q][:, js, :], in_=h_rows[q][:, js, :])
+
+        def load_c(q):
+            c_sb[q] = work.tile([P, CHUNK, H], BF16, name="c_sb", tag="c_sb", bufs=3)
+            nc.sync.dma_start(out=c_sb[q][:], in_=c_rows[q])
+
+        def gate_cols(g):
+            return slice(GATE_BLOCK[g] * H, (GATE_BLOCK[g] + 1) * H)
+
+        def spread_bias(g):
+            acc = mx_bank()
+            nc.tensor.matmul(out=acc[:], lhsT=ones[:], rhs=bias_rows[:, gate_cols(g)], start=True, stop=True)
+            nc.scalar.copy(out=bias_bc[g][:], in_=acc[:])
+
+        def prepare_wih(g):
+            acc = turn_tile()
+            view = acc[:].bitcast(BF16)
+            for half in range(2):
+                for j in range(4):
+                    col = half * H + j * P
+                    nc.tensor.transpose(view[:, col : col + P], wih_raw[g][:, j, half * P : (half + 1) * P], ident_bf[:])
+            nc.vector.tensor_copy(out=wih_t[g][:].rearrange("p a n -> p (a n)"), in_=view)
+
+        def turn_words(dst, rows):
+            words = rows.bitcast(F32)
+            for u in range(2):
+                nc.tensor.transpose(dst[:, u * P : (u + 1) * P], words[:, u : 2 * P : 2], ident_f32[:])
+
+        def prepare_whh(g):
+            grouped = words_tile()
+            grouped_words = grouped[:].bitcast(F32)
+            for pair in range(2):
+                acc = mx_bank()
+                for jj in range(2):
+                    turn_words(acc[:, jj * 2 * P : (jj + 1) * 2 * P], whh_raw[g][:, 2 * pair + jj, :])
+                nc.scalar.copy(
+                    out=grouped_words[:, pair * H : (pair + 1) * H].rearrange("p (j r u) -> p j r u", j=2, u=2),
+                    in_=acc[:].rearrange("p (j u r) -> p j r u", j=2, u=2),
+                )
+            nc.vector.quantize_mx(out=whh_codes[g][:].bitcast(E5M2X4), scales=whh_scales[g][:], in_=grouped[:])
+
+        def turn_steps(t):
+            q, j = divmod(t, CHUNK)
+
+            def turn_x(half):
+                if half == 0:
+                    turn_bank[t] = turn_tile()
+                view = turn_bank[t][:, 2 * P : 3 * P].bitcast(BF16)
+                nc.tensor.transpose(view[:, half * P : (half + 1) * P], x_sb[q][:, j, half * P : (half + 1) * P], ident_bf[:])
+
+            def turn_h(u):
+                words = h_sb[q][:, j, :].bitcast(F32)
+                nc.tensor.transpose(turn_bank[t][:, u * P : (u + 1) * P], words[:, u : 2 * P : 2], ident_f32[:])
+
+            return [lambda: turn_x(0), lambda: turn_x(1), lambda: turn_h(0), lambda: turn_h(1)]
+
+        def copy_turned(t):
+            q, j = divmod(t, CHUNK)
+            if j == 0:
+                x_tr[q] = work.tile([P, CHUNK, 2 * P], BF16, name="x_tr", tag="x_tr", bufs=3)
+                h_words[q] = words_tile()
+            acc = turn_bank[t]
+            nc.scalar.copy(out=x_tr[q][:, j, :], in_=acc[:, 2 * P : 3 * P].bitcast(BF16))
+            nc.scalar.copy(
+                out=h_words[q][:].bitcast(F32)[:, j * 2 * P : (j + 1) * 2 * P].rearrange("p (r u) -> p r u", u=2),
+                in_=acc[:, 0 : 2 * P].rearrange("p (u r) -> p r u", u=2),
+            )
+
+        def quantize_h(first, count):
+            q, j = divmod(first, CHUNK)
+            if j == 0:
+                h_codes[q] = work.tile([P, CHUNK * P], U32, name="h_codes", tag="h_codes", bufs=3, align_bytes=64)
+                h_scales[q] = work.tile([P, CHUNK * P], U8, name="h_scales", tag="h_scales", bufs=3, align_bytes=64)
+            cols = slice(j * P, (j + count) * P)
+            nc.vector.quantize_mx(
+                out=h_codes[q][:, cols].bitcast(E5M2X4),
+                scales=h_scales[q][:, cols],
+                in_=h_words[q][:, j * 4 * P : (j + count) * 4 * P],
+            )
+
+        def z_view(t, g):
+            if g == "f":
+                return z_fi[t][:, 0:H]
+            if g == "i":
+                return z_fi[t][:, H : 2 * H]
+            return z_o[t][:] if g == "o" else z_g[t][:]
+
+        def plain_product(t, g, between):
+            q, j = divmod(t, CHUNK)
+            on_scalar = g == "g"
+            acc = bank("plain_s", 1) if on_scalar else bank("plain_v", 2)
+            if on_scalar:
+                nc.tensor.matmul(out=acc[:], lhsT=ones[:], rhs=bias_rows[:, gate_cols(g)], start=True, stop=False)
+            nc.tensor.matmul(out=acc[:], lhsT=x_tr[q][:, j, 0:P], rhs=wih_t[g][:, 0, :], start=not on_scalar, stop=False)
+            for step in between:
+                step()
+            nc.tensor.matmul(out=acc[:], lhsT=x_tr[q][:, j, P : 2 * P], rhs=wih_t[g][:, 1, :], start=False, stop=True)
+            return acc
+
+        def plain_with_bias(t, g, between):
+            acc = plain_product(t, g, between)
+            nc.vector.tensor_tensor(out=z_view(t, g), in0=acc[:], in1=bias_bc[g][:], op=ALU.add)
+
+        def mx_product(t, g):
+            q, j = divmod(t, CHUNK)
+            cols = slice(j * P, (j + 1) * P)
+            acc = mx_bank()
+            nc.tensor.matmul_mx(
+                out=acc[:],
+                lhsT=h_codes[q][:, cols].bitcast(E5M2X4),
+                lhsT_scale=h_scales[q][:, cols],
+                rhs=whh_codes[g][:].bitcast(E5M2X4),
+                rhs_scale=whh_scales[g][:],
+                start=True,
+                stop=True,
+            )
+            nc.vector.tensor_tensor(out=z_view(t, g), in0=acc[:], in1=z_view(t, g), op=ALU.add)
+
+        def sigmoids(t):
+            s_fi[t] = fi_sized(F32, [P, 2 * H])
+            s_o[t] = o_sized(F32, [P, H])
+            nc.scalar.activation(out=s_fi[t][:], in_=z_fi[t][:], func=ACT.Sigmoid)
+            nc.scalar.activation(out=s_o[t][:], in_=z_o[t][:], func=ACT.Sigmoid)
+
+        def tanh_g(t):
+            t_g[t] = work.tile([P, H], F32, name="t_g", tag="t_g", bufs=LAG + 1)
+            nc.scalar.activation(out=t_g[t][:], in_=z_g[t][:], func=ACT.Tanh)
+
+        def tanh_c(t):
+            t_c[t] = work.tile([P, H], F32, name="t_c", tag="t_c", bufs=LAG + 1)
+            nc.scalar.activation(out=t_c[t][:], in_=c_new[t][:], func=ACT.Tanh)
+
+        def hidden(t, engine):
+            h_new = work.tile([P, H], F32, name="h_new", tag="h_new", bufs=3)
+            engine.tensor_tensor(out=h_new[:], in0=s_o[t][:], in1=t_c[t][:], op=ALU.mult)
+            nc.sync.dma_start(out=h_out[t // CHUNK, t % CHUNK], in_=h_new[:])
+
+        def cell(t):
+            q, j = divmod(t, CHUNK)
+            engine = nc.vector if t >= VECTOR_FROM else nc.gpsimd
+            fi = s_fi[t]
+            engine.tensor_tensor(out=fi[:, 0:H], in0=fi[:, 0:H], in1=c_sb[q][:, j, :], op=ALU.mult)
+            engine.tensor_tensor(out=fi[:, H : 2 * H], in0=fi[:, H : 2 * H], in1=t_g[t][:], op=ALU.mult)
+            if t >= LAG:
+                hidden(t - LAG, engine)
+            c_new[t] = work.tile([P, H], F32, name="c_new", tag="c_new", bufs=LAG + 2)
+            engine.tensor_tensor(out=c_new[t][:], in0=fi[:, 0:H], in1=fi[:, H : 2 * H], op=ALU.add)
+            nc.sync.dma_start(out=c_out[q, j], in_=c_new[t][:])
+            if j == 1 and q + 2 < CHUNKS and q >= 1:
+                load_c(q + 2)
+
+        def tiles_to_turn(t):
+            if t < RAMP:
+                return [2 * t + 2, 2 * t + 3]
+            return [t + AHEAD] if t + AHEAD < TILES else []
+
+        def step(t, prepare):
+            turned = tiles_to_turn(t)
+            turns = [s for tile_index in turned for s in turn_steps(tile_index)]
+            share = len(turns) // 4
+            between = [turns[n * share : (n + 1) * share] for n in range(4)]
+            z_fi[t] = work.tile([P, 2 * H], F32, name="z_fi", tag="z_fi", bufs=2)
+            z_o[t] = work.tile([P, H], F32, name="z_o", tag="z_o", bufs=2)
+            z_g[t] = work.tile([P, H], F32, name="z_g", tag="z_g", bufs=3)
+
+            plain_with_bias(t, "f", between[0])
+            prepare[0]()
+            if t >= 1:
+                mx_product(t - 1, "g")
+                if t - 1 >= LAG:
+                    tanh_c(t - 1 - LAG)
+                sigmoids(t - 1)
+            acc_g = plain_product(t, "g", between[1])
+            if t >= 1:
+                tanh_g(t - 1)
+            nc.scalar.copy(out=z_g[t][:], in_=acc_g[:])
+            if len(turned) == 2:
+                copy_turned(turned[0])
+            prepare[1]()
+            plain_with_bias(t, "i", between[2])
+            prepare[2]()
+            mx_product(t, "f")
+            if t == 1:
+                quantize_h(2, 2)
+            elif t % CHUNK == CHUNK - 1 and t + 1 < TILES:
+                quantize_h(t + 1, CHUNK)
+            prepare[3]()
+            plain_with_bias(t, "o", between[3])
+            mx_product(t, "i")
+            prepare[4]()
+            mx_product(t, "o")
+            if turned:
+                copy_turned(turned[-1])
+            if t >= 1 and t - 1 < VECTOR_FROM:
+                cell(t - 1)
+
+        nc.vector.memset(bias_rows[:].bitcast(I32), 0)
+        nc.vector.memset(ones[:], 1.0)
+        make_identity(nc, ident_bf[:])
+        make_identity(nc, ident_f32[:])
+        load_wih("f")
+        nc.sync.dma_start(out=bias_rows[0:1, :], in_=b_ih.rearrange("(o n) -> o n", o=1))
+        nc.sync.dma_start(out=bias_rows[1:2, :], in_=b_hh.rearrange("(o n) -> o n", o=1))
+        load_x(0, slice(0, 2))
+        load_whh("f")
+        load_h(0, slice(0, 2))
+        load_wih("g")
+        load_wih("i")
+        load_x(0, slice(2, 4))
+        load_h(0, slice(2, 4))
+        load_whh("i")
+        load_wih("o")
+        load_whh("o")
+        load_whh("g")
+        load_x(1)
+        load_h(1)
+        load_c(0)
+        load_x(2)
+        load_h(2)
+        load_c(1)
+        load_c(2)
+        for q in range(3, CHUNKS):
+            load_x(q)
+            load_h(q)
+
+        for g in "fio":
+            spread_bias(g)
+        prepare_wih("f")
+        prepare_whh("f")
+        for t in range(2):
+            for turn in turn_steps(t):
+                turn()
+            copy_turned(t)
+        quantize_h(0, 2)
+        prepare_wih("g")
+
+        step(
+            0,
+            [
+                lambda: prepare_wih("i"),
+                lambda: prepare_whh("i"),
+                lambda: prepare_wih("o"),
+                lambda: prepare_whh("o"),
+                lambda: prepare_whh("g"),
+            ],
+        )
+        for t in range(1, TILES):
+            step(t, [lambda: None] * 5)
+
+        last = TILES - 1
+        mx_product(last, "g")
+        tanh_c(last - LAG)
+        sigmoids(last)
+        tanh_g(last)
+        for t in range(VECTOR_FROM, TILES):
+            cell(t)
+        for t in range(TILES - LAG, TILES):
+            tanh_c(t)
+            hidden(t, nc.vector)

@@ -20,10 +20,10 @@ TILES = B // P
 CHUNK = 4
 CHUNKS = TILES // CHUNK
 GATE_BLOCK = {"i": 0, "f": 1, "g": 2, "o": 3}
-AHEAD = 5
-RAMP = 3
-LAG = 4
-VECTOR_FROM = 30
+GATE_FUNC = {"i": ACT.Sigmoid, "f": ACT.Sigmoid, "g": ACT.Tanh, "o": ACT.Sigmoid}
+TURNED_GATES = "igo"
+X_AHEAD = 2
+H_AHEAD = 9
 
 
 def tile_nodelstmcell_pa_t_kernel(tc, x_t, h, c, W_ih, W_hh, b_ih, b_hh, out_0, out_1):
@@ -46,48 +46,42 @@ def tile_nodelstmcell_pa_t_kernel(tc, x_t, h, c, W_ih, W_hh, b_ih, b_hh, out_0, 
         ident_f32 = keep.tile([P, P], F32, name="ident_f32")
         ones = keep.tile([P, P], BF16, name="ones")
         bias_rows = keep.tile([P, 4 * H], BF16, name="bias_rows")
-        bias_bc = {g: keep.tile([P, H], F32, name="bias_bc_" + g) for g in "fio"}
+        bias_f = keep.tile([P, H], F32, name="bias_f")
+        bias_cols = keep.tile([P, 16], F32, name="bias_cols")
         wih_t = {g: keep.tile([P, 2, H], BF16, name="wih_t_" + g) for g in "figo"}
         whh_codes = {g: keep.tile([P, H], U32, name="whh_codes_" + g, align_bytes=64) for g in "figo"}
         whh_scales = {g: keep.tile([P, H], U8, name="whh_scales_" + g, align_bytes=64) for g in "figo"}
+        whh_raw = {g: keep.tile([P, 4, H], BF16, name="whh_raw_" + g) for g in "figo"}
         x_sb = [keep.tile([P, CHUNK, I], BF16, name="x_sb%d" % q) for q in range(CHUNKS)]
         h_sb = [keep.tile([P, CHUNK, H], BF16, name="h_sb%d" % q) for q in range(CHUNKS)]
 
-        wih_raw, whh_raw, c_sb = {}, {}, {}
-        x_tr, h_words, h_codes, h_scales, turn_bank = {}, {}, {}, {}, {}
-        z_fi, z_o, z_g, s_fi, s_o, t_g, c_new, t_c = {}, {}, {}, {}, {}, {}, {}, {}
+        wih_raw, c_sb, x_tr, h_words, h_codes, h_scales = {}, {}, {}, {}, {}, {}
+        mx_t, z_f, gate, c_new, t_c = {}, {}, {}, {}, {}
 
-        def bank(tag, bufs, dtype=F32, width=H):
-            return psum.tile([P, width], dtype, name=tag, tag=tag, bufs=bufs)
+        def bank(tag, bufs):
+            return psum.tile([P, H], F32, name=tag, tag=tag, bufs=bufs)
 
-        def turn_tile():
-            return bank("turn", 2)
-
-        def mx_bank():
-            return bank("mx", 3)
+        def gate_bank():
+            return bank("gate", 3)
 
         def words_tile():
             return work.tile([P, 4 * H], BF16, name="words", tag="words", bufs=3, align_bytes=64)
 
-        def fi_sized(dtype, shape):
-            return work.tile(shape, dtype, name="s_fi", tag="s_fi", bufs=LAG + 1)
-
-        def o_sized(dtype, shape):
-            return work.tile(shape, dtype, name="s_o", tag="s_o", bufs=2 * LAG)
+        def mx_t_sized(dtype, shape):
+            return work.tile(shape, dtype, name="mx_t", tag="mx_t", bufs=2 * 4 * len(TURNED_GATES))
 
         def load_wih(g):
-            wih_raw[g] = o_sized(BF16, [P, 4, I])
+            wih_raw[g] = mx_t_sized(BF16, [P, 4, I])
             nc.sync.dma_start(out=wih_raw[g][:], in_=wih_rows[GATE_BLOCK[g]])
 
         def load_whh(g):
-            whh_raw[g] = fi_sized(BF16, [P, 4, H])
             nc.sync.dma_start(out=whh_raw[g][:], in_=whh_rows[GATE_BLOCK[g]])
 
-        def load_x(q, js=slice(0, CHUNK)):
-            nc.sync.dma_start(out=x_sb[q][:, js, :], in_=x_rows[q][:, js, :])
+        def load_x(q):
+            nc.sync.dma_start(out=x_sb[q][:], in_=x_rows[q])
 
-        def load_h(q, js=slice(0, CHUNK)):
-            nc.sync.dma_start(out=h_sb[q][:, js, :], in_=h_rows[q][:, js, :])
+        def load_h(q):
+            nc.sync.dma_start(out=h_sb[q][:], in_=h_rows[q])
 
         def load_c(q):
             c_sb[q] = work.tile([P, CHUNK, H], BF16, name="c_sb", tag="c_sb", bufs=3)
@@ -96,13 +90,19 @@ def tile_nodelstmcell_pa_t_kernel(tc, x_t, h, c, W_ih, W_hh, b_ih, b_hh, out_0, 
         def gate_cols(g):
             return slice(GATE_BLOCK[g] * H, (GATE_BLOCK[g] + 1) * H)
 
-        def spread_bias(g):
-            acc = mx_bank()
-            nc.tensor.matmul(out=acc[:], lhsT=ones[:], rhs=bias_rows[:, gate_cols(g)], start=True, stop=True)
-            nc.scalar.copy(out=bias_bc[g][:], in_=acc[:])
+        def spread_bias():
+            acc = bank("mx_f", 1)
+            nc.tensor.matmul(out=acc[:], lhsT=ones[:], rhs=bias_rows[:, gate_cols("f")], start=True, stop=True)
+            nc.scalar.copy(out=bias_f[:], in_=acc[:])
+            acc = bank("plain_f", 1)
+            for n in range(16):
+                nc.tensor.matmul(
+                    out=acc[:, n : n + 1], lhsT=bias_rows[:, n * P : (n + 1) * P], rhs=ones[:, 0:1], start=True, stop=True
+                )
+            nc.scalar.copy(out=bias_cols[:], in_=acc[:, 0:16])
 
-        def prepare_wih(g):
-            acc = turn_tile()
+        def prepare_wih(g, tag):
+            acc = bank(tag, 1)
             view = acc[:].bitcast(BF16)
             for half in range(2):
                 for j in range(4):
@@ -115,234 +115,253 @@ def tile_nodelstmcell_pa_t_kernel(tc, x_t, h, c, W_ih, W_hh, b_ih, b_hh, out_0, 
             for u in range(2):
                 nc.tensor.transpose(dst[:, u * P : (u + 1) * P], words[:, u : 2 * P : 2], ident_f32[:])
 
-        def prepare_whh(g):
+        def group_words(raw, copy):
             grouped = words_tile()
             grouped_words = grouped[:].bitcast(F32)
             for pair in range(2):
-                acc = mx_bank()
+                acc = gate_bank()
                 for jj in range(2):
-                    turn_words(acc[:, jj * 2 * P : (jj + 1) * 2 * P], whh_raw[g][:, 2 * pair + jj, :])
-                nc.scalar.copy(
+                    turn_words(acc[:, jj * 2 * P : (jj + 1) * 2 * P], raw[:, 2 * pair + jj, :])
+                copy(
                     out=grouped_words[:, pair * H : (pair + 1) * H].rearrange("p (j r u) -> p j r u", j=2, u=2),
                     in_=acc[:].rearrange("p (j u r) -> p j r u", j=2, u=2),
                 )
+            return grouped
+
+        def prepare_whh(g):
+            grouped = group_words(whh_raw[g], nc.scalar.copy)
             nc.vector.quantize_mx(out=whh_codes[g][:].bitcast(E5M2X4), scales=whh_scales[g][:], in_=grouped[:])
 
-        def turn_steps(t):
+        def quantize_h(q):
+            h_codes[q] = work.tile([P, CHUNK * P], U32, name="h_codes", tag="h_codes", bufs=3, align_bytes=64)
+            h_scales[q] = work.tile([P, CHUNK * P], U8, name="h_scales", tag="h_scales", bufs=3, align_bytes=64)
+            nc.vector.quantize_mx(out=h_codes[q][:].bitcast(E5M2X4), scales=h_scales[q][:], in_=h_words[q][:])
+
+        def prepare_h(q):
+            h_words[q] = group_words(h_sb[q], nc.vector.tensor_copy)
+            quantize_h(q)
+
+        def x_view(acc):
+            return acc[:, 2 * P : 3 * P].bitcast(BF16)
+
+        def turn_x(acc, t):
             q, j = divmod(t, CHUNK)
+            for half in range(2):
+                cols = slice(half * P, (half + 1) * P)
+                nc.tensor.transpose(x_view(acc)[:, cols], x_sb[q][:, j, cols], ident_bf[:])
 
-            def turn_x(half):
-                if half == 0:
-                    turn_bank[t] = turn_tile()
-                view = turn_bank[t][:, 2 * P : 3 * P].bitcast(BF16)
-                nc.tensor.transpose(view[:, half * P : (half + 1) * P], x_sb[q][:, j, half * P : (half + 1) * P], ident_bf[:])
+        def copy_x(acc, t):
+            x_tr[t] = work.tile([P, 2 * P], BF16, name="x_tr", tag="x_tr", bufs=X_AHEAD + 2)
+            nc.scalar.copy(out=x_tr[t][:], in_=x_view(acc))
 
-            def turn_h(u):
-                words = h_sb[q][:, j, :].bitcast(F32)
-                nc.tensor.transpose(turn_bank[t][:, u * P : (u + 1) * P], words[:, u : 2 * P : 2], ident_f32[:])
+        def turn_h(acc, t):
+            q, j = divmod(t, CHUNK)
+            turn_words(acc[:, 0 : 2 * P], h_sb[q][:, j, :])
 
-            return [lambda: turn_x(0), lambda: turn_x(1), lambda: turn_h(0), lambda: turn_h(1)]
-
-        def copy_turned(t):
+        def copy_h(acc, t):
             q, j = divmod(t, CHUNK)
             if j == 0:
-                x_tr[q] = work.tile([P, CHUNK, 2 * P], BF16, name="x_tr", tag="x_tr", bufs=3)
                 h_words[q] = words_tile()
-            acc = turn_bank[t]
-            nc.scalar.copy(out=x_tr[q][:, j, :], in_=acc[:, 2 * P : 3 * P].bitcast(BF16))
             nc.scalar.copy(
                 out=h_words[q][:].bitcast(F32)[:, j * 2 * P : (j + 1) * 2 * P].rearrange("p (r u) -> p r u", u=2),
                 in_=acc[:, 0 : 2 * P].rearrange("p (u r) -> p r u", u=2),
             )
 
-        def quantize_h(first, count):
-            q, j = divmod(first, CHUNK)
-            if j == 0:
-                h_codes[q] = work.tile([P, CHUNK * P], U32, name="h_codes", tag="h_codes", bufs=3, align_bytes=64)
-                h_scales[q] = work.tile([P, CHUNK * P], U8, name="h_scales", tag="h_scales", bufs=3, align_bytes=64)
-            cols = slice(j * P, (j + count) * P)
-            nc.vector.quantize_mx(
-                out=h_codes[q][:, cols].bitcast(E5M2X4),
-                scales=h_scales[q][:, cols],
-                in_=h_words[q][:, j * 4 * P : (j + count) * 4 * P],
+        def mx_turned(q, g, j):
+            cols = slice(j * P, (j + 1) * P)
+            acc = bank("mx_t", 2)
+            nc.tensor.matmul_mx(
+                out=acc[:],
+                lhsT=whh_codes[g][:, cols].bitcast(E5M2X4),
+                lhsT_scale=whh_scales[g][:, cols],
+                rhs=h_codes[q][:].bitcast(E5M2X4),
+                rhs_scale=h_scales[q][:],
+                start=True,
+                stop=True,
             )
-
-        def z_view(t, g):
-            if g == "f":
-                return z_fi[t][:, 0:H]
-            if g == "i":
-                return z_fi[t][:, H : 2 * H]
-            return z_o[t][:] if g == "o" else z_g[t][:]
-
-        def plain_product(t, g, between):
-            q, j = divmod(t, CHUNK)
-            on_scalar = g == "g"
-            acc = bank("plain_s", 1) if on_scalar else bank("plain_v", 2)
-            if on_scalar:
-                nc.tensor.matmul(out=acc[:], lhsT=ones[:], rhs=bias_rows[:, gate_cols(g)], start=True, stop=False)
-            nc.tensor.matmul(out=acc[:], lhsT=x_tr[q][:, j, 0:P], rhs=wih_t[g][:, 0, :], start=not on_scalar, stop=False)
-            for step in between:
-                step()
-            nc.tensor.matmul(out=acc[:], lhsT=x_tr[q][:, j, P : 2 * P], rhs=wih_t[g][:, 1, :], start=False, stop=True)
             return acc
 
-        def plain_with_bias(t, g, between):
-            acc = plain_product(t, g, between)
-            nc.vector.tensor_tensor(out=z_view(t, g), in0=acc[:], in1=bias_bc[g][:], op=ALU.add)
+        def empty_mx_turned(acc, q, g, j):
+            mx_t[q, g, j] = mx_t_sized(F32, [P, CHUNK * P])
+            n = GATE_BLOCK[g] * 4 + j
+            bias = bias_cols[:, n : n + 1]
+            if g == "i":
+                nc.vector.tensor_scalar(out=mx_t[q, g, j][:], in0=acc[:], scalar1=bias, scalar2=None, op0=ALU.add)
+            else:
+                nc.scalar.activation(out=mx_t[q, g, j][:], in_=acc[:], func=ACT.Identity, bias=bias)
 
-        def mx_product(t, g):
+        def plain_product(acc, t, g, between):
+            nc.tensor.matmul(out=acc[:], lhsT=x_tr[t][:, 0:P], rhs=wih_t[g][:, 0, :], start=True, stop=False)
+            between()
+            nc.tensor.matmul(out=acc[:], lhsT=x_tr[t][:, P : 2 * P], rhs=wih_t[g][:, 1, :], start=False, stop=True)
+
+        def turned_gate(t, g):
+            q, j = divmod(t, CHUNK)
+            acc = gate_bank()
+
+            def add_mx():
+                for block in range(4):
+                    nc.tensor.matmul(
+                        out=acc[:, block * P : (block + 1) * P],
+                        lhsT=mx_t[q, g, block][:, j * P : (j + 1) * P],
+                        rhs=ident_f32[:],
+                        is_transpose=True,
+                        start=False,
+                        stop=False,
+                    )
+
+            plain_product(acc, t, g, add_mx)
+            return acc
+
+        def mx_f(t):
             q, j = divmod(t, CHUNK)
             cols = slice(j * P, (j + 1) * P)
-            acc = mx_bank()
+            acc = bank("mx_f", 1)
             nc.tensor.matmul_mx(
                 out=acc[:],
                 lhsT=h_codes[q][:, cols].bitcast(E5M2X4),
                 lhsT_scale=h_scales[q][:, cols],
-                rhs=whh_codes[g][:].bitcast(E5M2X4),
-                rhs_scale=whh_scales[g][:],
+                rhs=whh_codes["f"][:].bitcast(E5M2X4),
+                rhs_scale=whh_scales["f"][:],
                 start=True,
                 stop=True,
             )
-            nc.vector.tensor_tensor(out=z_view(t, g), in0=acc[:], in1=z_view(t, g), op=ALU.add)
+            return acc
 
-        def sigmoids(t):
-            s_fi[t] = fi_sized(F32, [P, 2 * H])
-            s_o[t] = o_sized(F32, [P, H])
-            nc.scalar.activation(out=s_fi[t][:], in_=z_fi[t][:], func=ACT.Sigmoid)
-            nc.scalar.activation(out=s_o[t][:], in_=z_o[t][:], func=ACT.Sigmoid)
+        def activate(t, g, src):
+            gate[t, g] = work.tile([P, H], F32, name="gate_" + g, tag="gate_" + g, bufs=4 if g == "o" else 3)
+            nc.scalar.activation(out=gate[t, g][:], in_=src[:], func=GATE_FUNC[g])
 
-        def tanh_g(t):
-            t_g[t] = work.tile([P, H], F32, name="t_g", tag="t_g", bufs=LAG + 1)
-            nc.scalar.activation(out=t_g[t][:], in_=z_g[t][:], func=ACT.Tanh)
+        def forget_term(t):
+            q, j = divmod(t, CHUNK)
+            f = gate[t, "f"]
+            nc.vector.tensor_tensor(out=f[:], in0=f[:], in1=c_sb[q][:, j, :], op=ALU.mult)
 
-        def tanh_c(t):
-            t_c[t] = work.tile([P, H], F32, name="t_c", tag="t_c", bufs=LAG + 1)
-            nc.scalar.activation(out=t_c[t][:], in_=c_new[t][:], func=ACT.Tanh)
-
-        def hidden(t, engine):
-            h_new = work.tile([P, H], F32, name="h_new", tag="h_new", bufs=3)
-            engine.tensor_tensor(out=h_new[:], in0=s_o[t][:], in1=t_c[t][:], op=ALU.mult)
-            nc.sync.dma_start(out=h_out[t // CHUNK, t % CHUNK], in_=h_new[:])
+        def input_term(t):
+            nc.vector.tensor_tensor(out=gate[t, "i"][:], in0=gate[t, "i"][:], in1=gate[t, "g"][:], op=ALU.mult)
 
         def cell(t):
             q, j = divmod(t, CHUNK)
-            engine = nc.vector if t >= VECTOR_FROM else nc.gpsimd
-            fi = s_fi[t]
-            engine.tensor_tensor(out=fi[:, 0:H], in0=fi[:, 0:H], in1=c_sb[q][:, j, :], op=ALU.mult)
-            engine.tensor_tensor(out=fi[:, H : 2 * H], in0=fi[:, H : 2 * H], in1=t_g[t][:], op=ALU.mult)
-            if t >= LAG:
-                hidden(t - LAG, engine)
-            c_new[t] = work.tile([P, H], F32, name="c_new", tag="c_new", bufs=LAG + 2)
-            engine.tensor_tensor(out=c_new[t][:], in0=fi[:, 0:H], in1=fi[:, H : 2 * H], op=ALU.add)
+            c_new[t] = work.tile([P, H], F32, name="c_new", tag="c_new", bufs=4)
+            nc.vector.tensor_tensor(out=c_new[t][:], in0=gate[t, "f"][:], in1=gate[t, "i"][:], op=ALU.add)
             nc.sync.dma_start(out=c_out[q, j], in_=c_new[t][:])
-            if j == 1 and q + 2 < CHUNKS and q >= 1:
+            if j == 1 and q >= 1 and q + 2 < CHUNKS:
                 load_c(q + 2)
 
-        def tiles_to_turn(t):
-            if t < RAMP:
-                return [2 * t + 2, 2 * t + 3]
-            return [t + AHEAD] if t + AHEAD < TILES else []
+        def tanh_c(t):
+            t_c[t] = work.tile([P, H], F32, name="t_c", tag="t_c", bufs=2)
+            nc.scalar.activation(out=t_c[t][:], in_=c_new[t][:], func=ACT.Tanh)
 
-        def step(t, prepare):
-            turned = tiles_to_turn(t)
-            turns = [s for tile_index in turned for s in turn_steps(tile_index)]
-            share = len(turns) // 4
-            between = [turns[n * share : (n + 1) * share] for n in range(4)]
-            z_fi[t] = work.tile([P, 2 * H], F32, name="z_fi", tag="z_fi", bufs=2)
-            z_o[t] = work.tile([P, H], F32, name="z_o", tag="z_o", bufs=2)
-            z_g[t] = work.tile([P, H], F32, name="z_g", tag="z_g", bufs=3)
+        def hidden(t):
+            h_new = work.tile([P, H], F32, name="h_new", tag="h_new", bufs=3)
+            nc.vector.tensor_tensor(out=h_new[:], in0=gate[t, "o"][:], in1=t_c[t][:], op=ALU.mult)
+            nc.sync.dma_start(out=h_out[t // CHUNK, t % CHUNK], in_=h_new[:])
 
-            plain_with_bias(t, "f", between[0])
-            prepare[0]()
+        def step(t):
+            q, j = divmod(t, CHUNK)
+            next_chunk = q + 1 < CHUNKS
+            x_next, h_next = t + X_AHEAD, t + H_AHEAD
+            turn = bank("turn", 1) if x_next < TILES else None
+
+            def turn_inputs():
+                if x_next < TILES:
+                    turn_x(turn, x_next)
+                if h_next < TILES:
+                    turn_h(turn, h_next)
+
+            acc = bank("plain_f", 1)
+            plain_product(acc, t, "f", turn_inputs)
+            z_f[t] = work.tile([P, H], F32, name="z_f", tag="z_f", bufs=2)
+            nc.vector.tensor_tensor(out=z_f[t][:], in0=acc[:], in1=bias_f[:], op=ALU.add)
             if t >= 1:
-                mx_product(t - 1, "g")
-                if t - 1 >= LAG:
-                    tanh_c(t - 1 - LAG)
-                sigmoids(t - 1)
-            acc_g = plain_product(t, "g", between[1])
+                forget_term(t - 1)
+            acc = mx_f(t)
+            nc.vector.tensor_tensor(out=z_f[t][:], in0=acc[:], in1=z_f[t][:], op=ALU.add)
             if t >= 1:
-                tanh_g(t - 1)
-            nc.scalar.copy(out=z_g[t][:], in_=acc_g[:])
-            if len(turned) == 2:
-                copy_turned(turned[0])
-            prepare[1]()
-            plain_with_bias(t, "i", between[2])
-            prepare[2]()
-            mx_product(t, "f")
-            if t == 1:
-                quantize_h(2, 2)
-            elif t % CHUNK == CHUNK - 1 and t + 1 < TILES:
-                quantize_h(t + 1, CHUNK)
-            prepare[3]()
-            plain_with_bias(t, "o", between[3])
-            mx_product(t, "i")
-            prepare[4]()
-            mx_product(t, "o")
-            if turned:
-                copy_turned(turned[-1])
-            if t >= 1 and t - 1 < VECTOR_FROM:
+                input_term(t - 1)
+            if t >= 2:
+                tanh_c(t - 2)
+            activate(t, "f", z_f[t])
+            activate(t, "i", turned_gate(t, "i"))
+            if x_next < TILES:
+                copy_x(turn, x_next)
+            if h_next < TILES:
+                copy_h(turn, h_next)
+            if next_chunk:
+                empty_mx_turned(mx_turned(q + 1, "i", j), q + 1, "i", j)
+            if t >= 1:
                 cell(t - 1)
+            if t >= 2:
+                hidden(t - 2)
+            if j == CHUNK - 1 and q + 2 < CHUNKS:
+                quantize_h(q + 2)
+            activate(t, "g", turned_gate(t, "g"))
+            activate(t, "o", turned_gate(t, "o"))
+            if next_chunk:
+                for g in "go":
+                    empty_mx_turned(mx_turned(q + 1, g, j), q + 1, g, j)
 
         nc.vector.memset(bias_rows[:].bitcast(I32), 0)
         nc.vector.memset(ones[:], 1.0)
-        make_identity(nc, ident_bf[:])
         make_identity(nc, ident_f32[:])
-        load_wih("f")
+        make_identity(nc, ident_bf[:])
+        load_h(0)
         nc.sync.dma_start(out=bias_rows[0:1, :], in_=b_ih.rearrange("(o n) -> o n", o=1))
         nc.sync.dma_start(out=bias_rows[1:2, :], in_=b_hh.rearrange("(o n) -> o n", o=1))
-        load_x(0, slice(0, 2))
-        load_whh("f")
-        load_h(0, slice(0, 2))
-        load_wih("g")
+        for g in "igof":
+            load_whh(g)
+        load_wih("f")
+        load_x(0)
         load_wih("i")
-        load_x(0, slice(2, 4))
-        load_h(0, slice(2, 4))
-        load_whh("i")
-        load_wih("o")
-        load_whh("o")
-        load_whh("g")
-        load_x(1)
         load_h(1)
-        load_c(0)
-        load_x(2)
+        load_wih("g")
+        load_wih("o")
         load_h(2)
+        load_c(0)
+        load_x(1)
         load_c(1)
+        load_h(3)
+        load_x(2)
         load_c(2)
         for q in range(3, CHUNKS):
             load_x(q)
-            load_h(q)
+            if q + 1 < CHUNKS:
+                load_h(q + 1)
 
-        for g in "fio":
-            spread_bias(g)
-        prepare_wih("f")
+        def first_mx_turned(g):
+            for j in range(4):
+                empty_mx_turned(mx_turned(0, g, j), 0, g, j)
+
+        prepare_h(0)
+        spread_bias()
+        prepare_whh("i")
+        prepare_whh("g")
+        first_mx_turned("i")
+        prepare_whh("o")
+        first_mx_turned("g")
         prepare_whh("f")
-        for t in range(2):
-            for turn in turn_steps(t):
-                turn()
-            copy_turned(t)
-        quantize_h(0, 2)
-        prepare_wih("g")
+        first_mx_turned("o")
+        prepare_wih("f", "plain_f")
+        for t in range(X_AHEAD):
+            turn = bank("turn", 1)
+            turn_x(turn, t)
+            copy_x(turn, t)
+        prepare_wih("i", "mx_f")
+        prepare_h(1)
+        prepare_wih("g", "plain_f")
+        turn = bank("turn", 1)
+        turn_h(turn, H_AHEAD - 1)
+        copy_h(turn, H_AHEAD - 1)
+        prepare_wih("o", "mx_f")
 
-        step(
-            0,
-            [
-                lambda: prepare_wih("i"),
-                lambda: prepare_whh("i"),
-                lambda: prepare_wih("o"),
-                lambda: prepare_whh("o"),
-                lambda: prepare_whh("g"),
-            ],
-        )
-        for t in range(1, TILES):
-            step(t, [lambda: None] * 5)
+        for t in range(TILES):
+            step(t)
 
         last = TILES - 1
-        mx_product(last, "g")
-        tanh_c(last - LAG)
-        sigmoids(last)
-        tanh_g(last)
-        for t in range(VECTOR_FROM, TILES):
-            cell(t)
-        for t in range(TILES - LAG, TILES):
-            tanh_c(t)
-            hidden(t, nc.vector)
+        forget_term(last)
+        input_term(last)
+        tanh_c(last - 1)
+        cell(last)
+        hidden(last - 1)
+        tanh_c(last)
+        hidden(last)

@@ -21,9 +21,10 @@ CHUNK = 4
 CHUNKS = TILES // CHUNK
 GATE_BLOCK = {"i": 0, "f": 1, "g": 2, "o": 3}
 GATE_FUNC = {"i": ACT.Sigmoid, "f": ACT.Sigmoid, "g": ACT.Tanh, "o": ACT.Sigmoid}
-TURNED_GATES = "igo"
-X_AHEAD = 2
-H_AHEAD = 9
+TURNED_GATES = "ig"
+DIRECT_GATES = "fo"
+PAIRS = TILES // 2
+VECTOR_BLOCKS = 3
 
 
 def tile_nodelstmcell_pa_t_kernel(tc, x_t, h, c, W_ih, W_hh, b_ih, b_hh, out_0, out_1):
@@ -31,8 +32,8 @@ def tile_nodelstmcell_pa_t_kernel(tc, x_t, h, c, W_ih, W_hh, b_ih, b_hh, out_0, 
     x_rows = x_t.rearrange("(q p j) k -> q p j k", p=P, j=CHUNK)
     h_rows = h.rearrange("(q p j) k -> q p j k", p=P, j=CHUNK)
     c_rows = c.rearrange("(q p j) k -> q p j k", p=P, j=CHUNK)
-    h_out = out_0.rearrange("(q p j) k -> q j p k", p=P, j=CHUNK)
-    c_out = out_1.rearrange("(q p j) k -> q j p k", p=P, j=CHUNK)
+    h_out = out_0.rearrange("(q p j) k -> q p j k", p=P, j=CHUNK)
+    c_out = out_1.rearrange("(q p j) k -> q p j k", p=P, j=CHUNK)
     wih_rows = W_ih.rearrange("(g j p) k -> g p j k", p=P, j=4)
     whh_rows = W_hh.rearrange("(g j p) k -> g p j k", p=P, j=4)
 
@@ -46,23 +47,22 @@ def tile_nodelstmcell_pa_t_kernel(tc, x_t, h, c, W_ih, W_hh, b_ih, b_hh, out_0, 
         ident_f32 = keep.tile([P, P], F32, name="ident_f32")
         ones = keep.tile([P, P], BF16, name="ones")
         bias_rows = keep.tile([P, 4 * H], BF16, name="bias_rows")
-        bias_f = keep.tile([P, H], F32, name="bias_f")
-        bias_cols = keep.tile([P, 16], F32, name="bias_cols")
+        bias_spread = {g: keep.tile([P, H], F32, name="bias_spread_" + g) for g in DIRECT_GATES}
+        bias_cols = keep.tile([P, len(TURNED_GATES), 4], F32, name="bias_cols")
         wih_t = {g: keep.tile([P, 2, H], BF16, name="wih_t_" + g) for g in "figo"}
         whh_codes = {g: keep.tile([P, H], U32, name="whh_codes_" + g, align_bytes=64) for g in "figo"}
         whh_scales = {g: keep.tile([P, H], U8, name="whh_scales_" + g, align_bytes=64) for g in "figo"}
-        whh_raw = {g: keep.tile([P, 4, H], BF16, name="whh_raw_" + g) for g in "figo"}
         x_sb = [keep.tile([P, CHUNK, I], BF16, name="x_sb%d" % q) for q in range(CHUNKS)]
         h_sb = [keep.tile([P, CHUNK, H], BF16, name="h_sb%d" % q) for q in range(CHUNKS)]
 
-        wih_raw, c_sb, x_tr, h_words, h_codes, h_scales = {}, {}, {}, {}, {}, {}
-        mx_t, z_f, gate, c_new, t_c = {}, {}, {}, {}, {}
+        wih_raw, whh_raw, c_sb, x_tr, h_words, h_codes, h_scales = {}, {}, {}, {}, {}, {}, {}
+        mx_t, s_fo, s_i, t_g, c_new, t_c = {}, {}, {}, {}, {}, {}
 
-        def bank(tag, bufs):
-            return psum.tile([P, H], F32, name=tag, tag=tag, bufs=bufs)
+        def sum_bank():
+            return psum.tile([P, H], F32, name="sums", tag="sums", bufs=7)
 
-        def gate_bank():
-            return bank("gate", 3)
+        def turn_bank():
+            return psum.tile([P, H], F32, name="turn", tag="turn", bufs=1)
 
         def words_tile():
             return work.tile([P, 4 * H], BF16, name="words", tag="words", bufs=3, align_bytes=64)
@@ -70,18 +70,29 @@ def tile_nodelstmcell_pa_t_kernel(tc, x_t, h, c, W_ih, W_hh, b_ih, b_hh, out_0, 
         def mx_t_sized(dtype, shape):
             return work.tile(shape, dtype, name="mx_t", tag="mx_t", bufs=2 * 4 * len(TURNED_GATES))
 
+        def s_fo_sized(dtype, shape):
+            return work.tile(shape, dtype, name="s_fo", tag="s_fo", bufs=3)
+
+        def pair_tile(name, bufs):
+            return work.tile([P, 2, H], F32, name=name, tag=name, bufs=bufs)
+
+        for gates in (TURNED_GATES, DIRECT_GATES):
+            raw = s_fo_sized(BF16, [P, 2, 4, H])
+            for n, g in enumerate(gates):
+                whh_raw[g] = raw[:, n, :, :]
+
         def load_wih(g):
             wih_raw[g] = mx_t_sized(BF16, [P, 4, I])
             nc.sync.dma_start(out=wih_raw[g][:], in_=wih_rows[GATE_BLOCK[g]])
 
         def load_whh(g):
-            nc.sync.dma_start(out=whh_raw[g][:], in_=whh_rows[GATE_BLOCK[g]])
+            nc.sync.dma_start(out=whh_raw[g], in_=whh_rows[GATE_BLOCK[g]])
 
         def load_x(q):
             nc.sync.dma_start(out=x_sb[q][:], in_=x_rows[q])
 
-        def load_h(q):
-            nc.sync.dma_start(out=h_sb[q][:], in_=h_rows[q])
+        def load_h(q, js=slice(0, CHUNK)):
+            nc.sync.dma_start(out=h_sb[q][:, js, :], in_=h_rows[q][:, js, :])
 
         def load_c(q):
             c_sb[q] = work.tile([P, CHUNK, H], BF16, name="c_sb", tag="c_sb", bufs=3)
@@ -91,42 +102,67 @@ def tile_nodelstmcell_pa_t_kernel(tc, x_t, h, c, W_ih, W_hh, b_ih, b_hh, out_0, 
             return slice(GATE_BLOCK[g] * H, (GATE_BLOCK[g] + 1) * H)
 
         def spread_bias():
-            acc = bank("mx_f", 1)
-            nc.tensor.matmul(out=acc[:], lhsT=ones[:], rhs=bias_rows[:, gate_cols("f")], start=True, stop=True)
-            nc.scalar.copy(out=bias_f[:], in_=acc[:])
-            acc = bank("plain_f", 1)
-            for n in range(16):
-                nc.tensor.matmul(
-                    out=acc[:, n : n + 1], lhsT=bias_rows[:, n * P : (n + 1) * P], rhs=ones[:, 0:1], start=True, stop=True
-                )
-            nc.scalar.copy(out=bias_cols[:], in_=acc[:, 0:16])
+            for g in DIRECT_GATES:
+                acc = sum_bank()
+                nc.tensor.matmul(out=acc[:], lhsT=ones[:], rhs=bias_rows[:, gate_cols(g)], start=True, stop=True)
+                nc.scalar.copy(out=bias_spread[g][:], in_=acc[:])
+            acc = sum_bank()
+            for n, g in enumerate(TURNED_GATES):
+                for block in range(4):
+                    nc.tensor.matmul(
+                        out=acc[:, 4 * n + block : 4 * n + block + 1],
+                        lhsT=bias_rows[:, gate_cols(g)][:, block * P : (block + 1) * P],
+                        rhs=ones[:, 0:1],
+                        start=True,
+                        stop=True,
+                    )
+            nc.scalar.copy(out=bias_cols[:].rearrange("p g b -> p (g b)"), in_=acc[:, 0 : 4 * len(TURNED_GATES)])
 
-        def prepare_wih(g, tag):
-            acc = bank(tag, 1)
+        def plain_turns(acc, raw):
             view = acc[:].bitcast(BF16)
-            for half in range(2):
-                for j in range(4):
-                    col = half * H + j * P
-                    nc.tensor.transpose(view[:, col : col + P], wih_raw[g][:, j, half * P : (half + 1) * P], ident_bf[:])
-            nc.vector.tensor_copy(out=wih_t[g][:].rearrange("p a n -> p (a n)"), in_=view)
 
-        def turn_words(dst, rows):
-            words = rows.bitcast(F32)
-            for u in range(2):
-                nc.tensor.transpose(dst[:, u * P : (u + 1) * P], words[:, u : 2 * P : 2], ident_f32[:])
+            def turn(half, j):
+                col = half * H + j * P
+                nc.tensor.transpose(view[:, col : col + P], raw[:, j, half * P : (half + 1) * P], ident_bf[:])
+
+            return [lambda half=half, j=j: turn(half, j) for half in range(2) for j in range(4)]
+
+        def copy_plain(dst, acc):
+            nc.scalar.copy(out=dst[:].rearrange("p a n -> p (a n)"), in_=acc[:].bitcast(BF16))
+
+        def word_turns(acc, raw, pair):
+            def turn(jj, u):
+                words = raw[:, 2 * pair + jj, :].bitcast(F32)
+                col = (2 * jj + u) * P
+                nc.tensor.transpose(acc[:, col : col + P], words[:, u : 2 * P : 2], ident_f32[:])
+
+            return [lambda jj=jj, u=u: turn(jj, u) for jj in range(2) for u in range(2)]
+
+        def copy_words(grouped, acc, pair, copy):
+            copy(
+                out=grouped[:].bitcast(F32)[:, pair * H : (pair + 1) * H].rearrange("p (j r u) -> p j r u", j=2, u=2),
+                in_=acc[:].rearrange("p (j u r) -> p j r u", j=2, u=2),
+            )
+
+        def run(steps):
+            for one in steps:
+                one()
+
+        def turn_plain(dst, raw):
+            acc = sum_bank()
+            run(plain_turns(acc, raw))
+            copy_plain(dst, acc)
 
         def group_words(raw, copy):
             grouped = words_tile()
-            grouped_words = grouped[:].bitcast(F32)
             for pair in range(2):
-                acc = gate_bank()
-                for jj in range(2):
-                    turn_words(acc[:, jj * 2 * P : (jj + 1) * 2 * P], raw[:, 2 * pair + jj, :])
-                copy(
-                    out=grouped_words[:, pair * H : (pair + 1) * H].rearrange("p (j r u) -> p j r u", j=2, u=2),
-                    in_=acc[:].rearrange("p (j u r) -> p j r u", j=2, u=2),
-                )
+                acc = sum_bank()
+                run(word_turns(acc, raw, pair))
+                copy_words(grouped, acc, pair, copy)
             return grouped
+
+        def prepare_wih(g):
+            turn_plain(wih_t[g], wih_raw[g])
 
         def prepare_whh(g):
             grouped = group_words(whh_raw[g], nc.scalar.copy)
@@ -141,184 +177,182 @@ def tile_nodelstmcell_pa_t_kernel(tc, x_t, h, c, W_ih, W_hh, b_ih, b_hh, out_0, 
             h_words[q] = group_words(h_sb[q], nc.vector.tensor_copy)
             quantize_h(q)
 
-        def x_view(acc):
-            return acc[:, 2 * P : 3 * P].bitcast(BF16)
+        def x_tr_tile():
+            return work.tile([P, 2, H], BF16, name="x_tr", tag="x_tr", bufs=2)
 
-        def turn_x(acc, t):
+        def input_turns(t):
             q, j = divmod(t, CHUNK)
-            for half in range(2):
-                cols = slice(half * P, (half + 1) * P)
-                nc.tensor.transpose(x_view(acc)[:, cols], x_sb[q][:, j, cols], ident_bf[:])
+            if j == 1 and q + 1 < CHUNKS:
+                acc = turn_bank()
+                x_tr[q + 1] = x_tr_tile()
+                return plain_turns(acc, x_sb[q + 1]), lambda: copy_plain(x_tr[q + 1], acc)
+            if j % 2 == 0 and q + 2 < CHUNKS:
+                acc = turn_bank()
+                if j == 0:
+                    h_words[q + 2] = words_tile()
+                return word_turns(acc, h_sb[q + 2], j // 2), lambda: copy_words(h_words[q + 2], acc, j // 2, nc.scalar.copy)
+            return [], lambda: None
 
-        def copy_x(acc, t):
-            x_tr[t] = work.tile([P, 2 * P], BF16, name="x_tr", tag="x_tr", bufs=X_AHEAD + 2)
-            nc.scalar.copy(out=x_tr[t][:], in_=x_view(acc))
-
-        def turn_h(acc, t):
-            q, j = divmod(t, CHUNK)
-            turn_words(acc[:, 0 : 2 * P], h_sb[q][:, j, :])
-
-        def copy_h(acc, t):
-            q, j = divmod(t, CHUNK)
-            if j == 0:
-                h_words[q] = words_tile()
-            nc.scalar.copy(
-                out=h_words[q][:].bitcast(F32)[:, j * 2 * P : (j + 1) * 2 * P].rearrange("p (r u) -> p r u", u=2),
-                in_=acc[:, 0 : 2 * P].rearrange("p (u r) -> p r u", u=2),
-            )
-
-        def mx_turned(q, g, j):
-            cols = slice(j * P, (j + 1) * P)
-            acc = bank("mx_t", 2)
+        def mx_product(stationary, moving):
+            acc = sum_bank()
             nc.tensor.matmul_mx(
                 out=acc[:],
-                lhsT=whh_codes[g][:, cols].bitcast(E5M2X4),
-                lhsT_scale=whh_scales[g][:, cols],
-                rhs=h_codes[q][:].bitcast(E5M2X4),
-                rhs_scale=h_scales[q][:],
+                lhsT=stationary[0].bitcast(E5M2X4),
+                lhsT_scale=stationary[1],
+                rhs=moving[0].bitcast(E5M2X4),
+                rhs_scale=moving[1],
                 start=True,
                 stop=True,
             )
             return acc
 
-        def empty_mx_turned(acc, q, g, j):
-            mx_t[q, g, j] = mx_t_sized(F32, [P, CHUNK * P])
-            n = GATE_BLOCK[g] * 4 + j
-            bias = bias_cols[:, n : n + 1]
-            if g == "i":
-                nc.vector.tensor_scalar(out=mx_t[q, g, j][:], in0=acc[:], scalar1=bias, scalar2=None, op0=ALU.add)
+        def mx_turned(q, g, block):
+            cols = slice(block * P, (block + 1) * P)
+            acc = mx_product((whh_codes[g][:, cols], whh_scales[g][:, cols]), (h_codes[q][:], h_scales[q][:]))
+            mx_t[q, g, block] = mx_t_sized(F32, [P, CHUNK * P])
+            bias = bias_cols[:, TURNED_GATES.index(g), block : block + 1]
+            if g == "i" and block < VECTOR_BLOCKS:
+                nc.vector.tensor_scalar(out=mx_t[q, g, block][:], in0=acc[:], scalar1=bias, scalar2=None, op0=ALU.add)
             else:
-                nc.scalar.activation(out=mx_t[q, g, j][:], in_=acc[:], func=ACT.Identity, bias=bias)
+                nc.scalar.activation(out=mx_t[q, g, block][:], in_=acc[:], func=ACT.Identity, bias=bias)
 
-        def plain_product(acc, t, g, between):
-            nc.tensor.matmul(out=acc[:], lhsT=x_tr[t][:, 0:P], rhs=wih_t[g][:, 0, :], start=True, stop=False)
-            between()
-            nc.tensor.matmul(out=acc[:], lhsT=x_tr[t][:, P : 2 * P], rhs=wih_t[g][:, 1, :], start=False, stop=True)
-
-        def turned_gate(t, g):
-            q, j = divmod(t, CHUNK)
-            acc = gate_bank()
-
-            def add_mx():
-                for block in range(4):
-                    nc.tensor.matmul(
-                        out=acc[:, block * P : (block + 1) * P],
-                        lhsT=mx_t[q, g, block][:, j * P : (j + 1) * P],
-                        rhs=ident_f32[:],
-                        is_transpose=True,
-                        start=False,
-                        stop=False,
-                    )
-
-            plain_product(acc, t, g, add_mx)
-            return acc
-
-        def mx_f(t):
+        def plain_product(t, g, between, behind):
             q, j = divmod(t, CHUNK)
             cols = slice(j * P, (j + 1) * P)
-            acc = bank("mx_f", 1)
-            nc.tensor.matmul_mx(
-                out=acc[:],
-                lhsT=h_codes[q][:, cols].bitcast(E5M2X4),
-                lhsT_scale=h_scales[q][:, cols],
-                rhs=whh_codes["f"][:].bitcast(E5M2X4),
-                rhs_scale=whh_scales["f"][:],
-                start=True,
-                stop=True,
-            )
+            acc = sum_bank()
+            closes = g in DIRECT_GATES
+            nc.tensor.matmul(out=acc[:], lhsT=x_tr[q][:, 0, cols], rhs=wih_t[g][:, 0, :], start=True, stop=False)
+            run(between(acc))
+            nc.tensor.matmul(out=acc[:], lhsT=x_tr[q][:, 1, cols], rhs=wih_t[g][:, 1, :], start=False, stop=closes)
+            run(behind(acc))
             return acc
 
-        def activate(t, g, src):
-            gate[t, g] = work.tile([P, H], F32, name="gate_" + g, tag="gate_" + g, bufs=4 if g == "o" else 3)
-            nc.scalar.activation(out=gate[t, g][:], in_=src[:], func=GATE_FUNC[g])
-
-        def forget_term(t):
+        def turned_gate(t, g, dst):
             q, j = divmod(t, CHUNK)
-            f = gate[t, "f"]
-            nc.vector.tensor_tensor(out=f[:], in0=f[:], in1=c_sb[q][:, j, :], op=ALU.mult)
 
-        def input_term(t):
-            nc.vector.tensor_tensor(out=gate[t, "i"][:], in0=gate[t, "i"][:], in1=gate[t, "g"][:], op=ALU.mult)
+            def add_mx(acc, block):
+                nc.tensor.matmul(
+                    out=acc[:, block * P : (block + 1) * P],
+                    lhsT=mx_t[q, g, block][:, j * P : (j + 1) * P],
+                    rhs=ident_f32[:],
+                    is_transpose=True,
+                    start=False,
+                    stop=block == 3,
+                )
 
-        def cell(t):
+            acc = plain_product(
+                t,
+                g,
+                lambda acc: [lambda: add_mx(acc, 0), lambda: add_mx(acc, 1)],
+                lambda acc: [lambda: add_mx(acc, 2), lambda: add_mx(acc, 3)],
+            )
+            nc.scalar.activation(out=dst, in_=acc[:], func=GATE_FUNC[g])
+
+        def direct_plain(t, g, z, between, behind):
+            acc = plain_product(t, g, lambda acc: between, lambda acc: behind)
+            nc.vector.tensor_tensor(out=z, in0=acc[:], in1=bias_spread[g][:], op=ALU.add)
+
+        def direct_mx(t, g, z):
             q, j = divmod(t, CHUNK)
-            c_new[t] = work.tile([P, H], F32, name="c_new", tag="c_new", bufs=4)
-            nc.vector.tensor_tensor(out=c_new[t][:], in0=gate[t, "f"][:], in1=gate[t, "i"][:], op=ALU.add)
-            nc.sync.dma_start(out=c_out[q, j], in_=c_new[t][:])
-            if j == 1 and q >= 1 and q + 2 < CHUNKS:
+            cols = slice(j * P, (j + 1) * P)
+            acc = mx_product((h_codes[q][:, cols], h_scales[q][:, cols]), (whh_codes[g][:], whh_scales[g][:]))
+            nc.vector.tensor_tensor(out=z, in0=acc[:], in1=z, op=ALU.add)
+
+        def gates_of_tile(t, prepare, scalar_meanwhile):
+            q, j = divmod(t, CHUNK)
+            s, n = divmod(t, 2)
+            turns, copy_turned = input_turns(t)
+            z = pair_tile("z_fo", 2)
+            turned_gate(t, "i", s_i[s][:, n, :])
+            scalar_meanwhile()
+            prepare[0]()
+            direct_plain(t, "f", z[:, 0, :], turns[0::3], turns[1::3])
+            prepare[1]()
+            turned_gate(t, "g", t_g[s][:, n, :])
+            prepare[2]()
+            direct_plain(t, "o", z[:, 1, :], turns[2::3], [])
+            if q + 1 < CHUNKS:
+                mx_turned(q + 1, "g", j)
+            copy_turned()
+            direct_mx(t, "f", z[:, 0, :])
+            direct_mx(t, "o", z[:, 1, :])
+            if q + 1 < CHUNKS:
+                mx_turned(q + 1, "i", j)
+            return lambda: nc.scalar.activation(out=s_fo[s][:, :, n, :], in_=z[:], func=ACT.Sigmoid)
+
+        def rows_of_pair(s):
+            q, half = divmod(s, 2)
+            return q, slice(2 * half, 2 * half + 2)
+
+        def input_term(s):
+            nc.vector.tensor_tensor(out=s_i[s][:], in0=s_i[s][:], in1=t_g[s][:], op=ALU.mult)
+
+        def forget_term(s):
+            q, js = rows_of_pair(s)
+            nc.vector.tensor_tensor(out=s_fo[s][:, 0, :, :], in0=s_fo[s][:, 0, :, :], in1=c_sb[q][:, js, :], op=ALU.mult)
+            if s % 2 == 0 and q >= 1 and q + 2 < CHUNKS:
                 load_c(q + 2)
 
-        def tanh_c(t):
-            t_c[t] = work.tile([P, H], F32, name="t_c", tag="t_c", bufs=2)
-            nc.scalar.activation(out=t_c[t][:], in_=c_new[t][:], func=ACT.Tanh)
+        def cell(s, engine, ns=slice(0, 2)):
+            q, js = rows_of_pair(s)
+            if ns.start == 0:
+                c_new[s] = pair_tile("c_new", 3)
+            engine.tensor_tensor(out=c_new[s][:, ns, :], in0=s_fo[s][:, 0, ns, :], in1=s_i[s][:, ns, :], op=ALU.add)
+            nc.sync.dma_start(out=c_out[q][:, js, :][:, ns, :], in_=c_new[s][:, ns, :])
 
-        def hidden(t):
-            h_new = work.tile([P, H], F32, name="h_new", tag="h_new", bufs=3)
-            nc.vector.tensor_tensor(out=h_new[:], in0=gate[t, "o"][:], in1=t_c[t][:], op=ALU.mult)
-            nc.sync.dma_start(out=h_out[t // CHUNK, t % CHUNK], in_=h_new[:])
+        def tanh_c(s, ns=slice(0, 2)):
+            if ns.start == 0:
+                t_c[s] = pair_tile("t_c", 2)
+            nc.scalar.activation(out=t_c[s][:, ns, :], in_=c_new[s][:, ns, :], func=ACT.Tanh)
 
-        def step(t):
-            q, j = divmod(t, CHUNK)
-            next_chunk = q + 1 < CHUNKS
-            x_next, h_next = t + X_AHEAD, t + H_AHEAD
-            turn = bank("turn", 1) if x_next < TILES else None
+        def hidden(s, engine, ns=slice(0, 2)):
+            q, js = rows_of_pair(s)
+            h_new = pair_tile("h_new", 2)
+            engine.tensor_tensor(out=h_new[:, ns, :], in0=s_fo[s][:, 1, ns, :], in1=t_c[s][:, ns, :], op=ALU.mult)
+            nc.sync.dma_start(out=h_out[q][:, js, :][:, ns, :], in_=h_new[:, ns, :])
 
-            def turn_inputs():
-                if x_next < TILES:
-                    turn_x(turn, x_next)
-                if h_next < TILES:
-                    turn_h(turn, h_next)
+        nothing = [lambda: None] * 3
 
-            acc = bank("plain_f", 1)
-            plain_product(acc, t, "f", turn_inputs)
-            z_f[t] = work.tile([P, H], F32, name="z_f", tag="z_f", bufs=2)
-            nc.vector.tensor_tensor(out=z_f[t][:], in0=acc[:], in1=bias_f[:], op=ALU.add)
-            if t >= 1:
-                forget_term(t - 1)
-            acc = mx_f(t)
-            nc.vector.tensor_tensor(out=z_f[t][:], in0=acc[:], in1=z_f[t][:], op=ALU.add)
-            if t >= 1:
-                input_term(t - 1)
-            if t >= 2:
-                tanh_c(t - 2)
-            activate(t, "f", z_f[t])
-            activate(t, "i", turned_gate(t, "i"))
-            if x_next < TILES:
-                copy_x(turn, x_next)
-            if h_next < TILES:
-                copy_h(turn, h_next)
-            if next_chunk:
-                empty_mx_turned(mx_turned(q + 1, "i", j), q + 1, "i", j)
-            if t >= 1:
-                cell(t - 1)
-            if t >= 2:
-                hidden(t - 2)
-            if j == CHUNK - 1 and q + 2 < CHUNKS:
-                quantize_h(q + 2)
-            activate(t, "g", turned_gate(t, "g"))
-            activate(t, "o", turned_gate(t, "o"))
-            if next_chunk:
-                for g in "go":
-                    empty_mx_turned(mx_turned(q + 1, g, j), q + 1, g, j)
+        def step(s, prepare):
+            q, half = divmod(s, 2)
+            if half == 0 and q >= 1 and q + 1 < CHUNKS:
+                quantize_h(q + 1)
+            if s >= 1:
+                input_term(s - 1)
+                forget_term(s - 1)
+            if s >= 2:
+                tanh_c(s - 2)
+            if s >= 1:
+                cell(s - 1, nc.gpsimd)
+            if s >= 2:
+                hidden(s - 2, nc.gpsimd)
+            s_i[s] = pair_tile("s_i", 2)
+            t_g[s] = pair_tile("t_g", 2)
+            s_fo[s] = s_fo_sized(F32, [P, 2, 2, H])
+            first_sigmoids = gates_of_tile(2 * s, prepare, lambda: None)
+            gates_of_tile(2 * s + 1, nothing, first_sigmoids)()
 
         nc.vector.memset(bias_rows[:].bitcast(I32), 0)
         nc.vector.memset(ones[:], 1.0)
         make_identity(nc, ident_f32[:])
         make_identity(nc, ident_bf[:])
-        load_h(0)
+        load_h(0, slice(0, 2))
+        load_h(0, slice(2, 4))
         nc.sync.dma_start(out=bias_rows[0:1, :], in_=b_ih.rearrange("(o n) -> o n", o=1))
         nc.sync.dma_start(out=bias_rows[1:2, :], in_=b_hh.rearrange("(o n) -> o n", o=1))
-        for g in "igof":
-            load_whh(g)
-        load_wih("f")
-        load_x(0)
+        load_whh("i")
+        load_whh("g")
         load_wih("i")
-        load_h(1)
+        load_x(0)
+        load_wih("f")
         load_wih("g")
+        load_whh("f")
         load_wih("o")
+        load_h(1)
+        load_whh("o")
         load_h(2)
-        load_c(0)
         load_x(1)
+        load_c(0)
         load_c(1)
         load_h(3)
         load_x(2)
@@ -328,40 +362,38 @@ def tile_nodelstmcell_pa_t_kernel(tc, x_t, h, c, W_ih, W_hh, b_ih, b_hh, out_0, 
             if q + 1 < CHUNKS:
                 load_h(q + 1)
 
-        def first_mx_turned(g):
-            for j in range(4):
-                empty_mx_turned(mx_turned(0, g, j), 0, g, j)
-
         prepare_h(0)
         spread_bias()
         prepare_whh("i")
         prepare_whh("g")
-        first_mx_turned("i")
-        prepare_whh("o")
-        first_mx_turned("g")
-        prepare_whh("f")
-        first_mx_turned("o")
-        prepare_wih("f", "plain_f")
-        for t in range(X_AHEAD):
-            turn = bank("turn", 1)
-            turn_x(turn, t)
-            copy_x(turn, t)
-        prepare_wih("i", "mx_f")
-        prepare_h(1)
-        prepare_wih("g", "plain_f")
-        turn = bank("turn", 1)
-        turn_h(turn, H_AHEAD - 1)
-        copy_h(turn, H_AHEAD - 1)
-        prepare_wih("o", "mx_f")
+        x_tr[0] = x_tr_tile()
+        head_turns = [
+            lambda: prepare_wih("i"),
+            lambda: turn_plain(x_tr[0], x_sb[0]),
+            lambda: prepare_wih("f"),
+            lambda: prepare_wih("g"),
+        ]
+        for n, turn_operand in enumerate(head_turns):
+            for block in (2 * n % 4, 2 * n % 4 + 1):
+                mx_turned(0, TURNED_GATES[n // 2], block)
+            turn_operand()
 
-        for t in range(TILES):
-            step(t)
+        def wih_o_and_h1():
+            prepare_wih("o")
+            prepare_h(1)
 
-        last = TILES - 1
-        forget_term(last)
-        input_term(last)
+        step(0, [lambda: prepare_whh("f"), wih_o_and_h1, lambda: prepare_whh("o")])
+        for s in range(1, PAIRS):
+            step(s, nothing)
+
+        last = PAIRS - 1
         tanh_c(last - 1)
-        cell(last)
-        hidden(last - 1)
-        tanh_c(last)
-        hidden(last)
+        input_term(last)
+        hidden(last - 1, nc.vector)
+        forget_term(last)
+        halves = [slice(0, 1), slice(1, 2)]
+        for ns in halves:
+            cell(last, nc.vector, ns)
+            tanh_c(last, ns)
+        for ns in halves:
+            hidden(last, nc.vector, ns)

@@ -16,15 +16,21 @@ ACT = mybir.ActivationFunctionType
 ALU = mybir.AluOpType
 
 P = 128
-TILES = B // P
 CHUNK = 4
+BLOCKS = H // P
+TILES = B // P
+PAIRS = TILES // 2
 CHUNKS = TILES // CHUNK
-GATE_BLOCK = {"i": 0, "f": 1, "g": 2, "o": 3}
-GATE_FUNC = {"i": ACT.Sigmoid, "f": ACT.Sigmoid, "g": ACT.Tanh, "o": ACT.Sigmoid}
+GATES = "ifgo"
 TURNED_GATES = "ig"
 DIRECT_GATES = "fo"
-PAIRS = TILES // 2
+TURNED_FUNC = {"i": ACT.Sigmoid, "g": ACT.Tanh}
 VECTOR_BLOCKS = 3
+
+
+def run(steps):
+    for one_step in steps:
+        one_step()
 
 
 def tile_nodelstmcell_pa_t_kernel(tc, x_t, h, c, W_ih, W_hh, b_ih, b_hh, out_0, out_1):
@@ -34,29 +40,33 @@ def tile_nodelstmcell_pa_t_kernel(tc, x_t, h, c, W_ih, W_hh, b_ih, b_hh, out_0, 
     c_rows = c.rearrange("(q p j) k -> q p j k", p=P, j=CHUNK)
     h_out = out_0.rearrange("(q p j) k -> q p j k", p=P, j=CHUNK)
     c_out = out_1.rearrange("(q p j) k -> q p j k", p=P, j=CHUNK)
-    wih_rows = W_ih.rearrange("(g j p) k -> g p j k", p=P, j=4)
-    whh_rows = W_hh.rearrange("(g j p) k -> g p j k", p=P, j=4)
+    wih_rows = W_ih.rearrange("(g j p) k -> g p j k", p=P, j=BLOCKS)
+    whh_rows = W_hh.rearrange("(g j p) k -> g p j k", p=P, j=BLOCKS)
 
     with ExitStack() as ctx:
         keep = ctx.enter_context(tc.tile_pool(name="keep", bufs=1))
         work = ctx.enter_context(tc.tile_pool(name="work", bufs=2))
         psum = ctx.enter_context(tc.psum_pool(name="psum", bufs=1))
         ctx.enter_context(tc.manual_schedule())
+        on_scalar, on_vector = nc.scalar.copy, nc.vector.tensor_copy
 
         ident_bf = keep.tile([P, P], BF16, name="ident_bf")
         ident_f32 = keep.tile([P, P], F32, name="ident_f32")
         ones = keep.tile([P, P], BF16, name="ones")
         bias_rows = keep.tile([P, 4 * H], BF16, name="bias_rows")
         bias_spread = {g: keep.tile([P, H], F32, name="bias_spread_" + g) for g in DIRECT_GATES}
-        bias_cols = keep.tile([P, len(TURNED_GATES), 4], F32, name="bias_cols")
-        wih_t = {g: keep.tile([P, 2, H], BF16, name="wih_t_" + g) for g in "figo"}
-        whh_codes = {g: keep.tile([P, H], U32, name="whh_codes_" + g, align_bytes=64) for g in "figo"}
-        whh_scales = {g: keep.tile([P, H], U8, name="whh_scales_" + g, align_bytes=64) for g in "figo"}
+        bias_cols = keep.tile([P, len(TURNED_GATES), BLOCKS], F32, name="bias_cols")
+        wih_t = {g: keep.tile([P, 2, H], BF16, name="wih_t_" + g) for g in GATES}
+        whh_codes = {g: keep.tile([P, H], U32, name="whh_codes_" + g, align_bytes=64) for g in GATES}
+        whh_scales = {g: keep.tile([P, H], U8, name="whh_scales_" + g, align_bytes=64) for g in GATES}
         x_sb = [keep.tile([P, CHUNK, I], BF16, name="x_sb%d" % q) for q in range(CHUNKS)]
         h_sb = [keep.tile([P, CHUNK, H], BF16, name="h_sb%d" % q) for q in range(CHUNKS)]
 
-        wih_raw, whh_raw, c_sb, x_tr, h_words, h_codes, h_scales = {}, {}, {}, {}, {}, {}, {}
-        mx_t, s_fo, s_i, t_g, c_new, t_c = {}, {}, {}, {}, {}, {}
+        wih_raw, whh_raw = {}, {}
+        c_sb, x_tr, h_words, h_codes, h_scales = {}, {}, {}, {}, {}
+        mx_t = {}
+        z_fo = {}
+        s_fo, s_i, t_g, c_new, t_c = {}, {}, {}, {}, {}
 
         def sum_bank():
             return psum.tile([P, H], F32, name="sums", tag="sums", bufs=7)
@@ -68,7 +78,7 @@ def tile_nodelstmcell_pa_t_kernel(tc, x_t, h, c, W_ih, W_hh, b_ih, b_hh, out_0, 
             return work.tile([P, 4 * H], BF16, name="words", tag="words", bufs=3, align_bytes=64)
 
         def mx_t_sized(dtype, shape):
-            return work.tile(shape, dtype, name="mx_t", tag="mx_t", bufs=2 * 4 * len(TURNED_GATES))
+            return work.tile(shape, dtype, name="mx_t", tag="mx_t", bufs=2 * BLOCKS * len(TURNED_GATES))
 
         def s_fo_sized(dtype, shape):
             return work.tile(shape, dtype, name="s_fo", tag="s_fo", bufs=3)
@@ -77,46 +87,49 @@ def tile_nodelstmcell_pa_t_kernel(tc, x_t, h, c, W_ih, W_hh, b_ih, b_hh, out_0, 
             return work.tile([P, 2, H], F32, name=name, tag=name, bufs=bufs)
 
         for gates in (TURNED_GATES, DIRECT_GATES):
-            raw = s_fo_sized(BF16, [P, 2, 4, H])
-            for n, g in enumerate(gates):
-                whh_raw[g] = raw[:, n, :, :]
+            two_gates = s_fo_sized(BF16, [P, 2, BLOCKS, H])
+            for place, g in enumerate(gates):
+                whh_raw[g] = two_gates[:, place, :, :]
 
         def load_wih(g):
-            wih_raw[g] = mx_t_sized(BF16, [P, 4, I])
-            nc.sync.dma_start(out=wih_raw[g][:], in_=wih_rows[GATE_BLOCK[g]])
+            wih_raw[g] = mx_t_sized(BF16, [P, BLOCKS, I])
+            nc.sync.dma_start(out=wih_raw[g][:], in_=wih_rows[GATES.index(g)])
 
         def load_whh(g):
-            nc.sync.dma_start(out=whh_raw[g], in_=whh_rows[GATE_BLOCK[g]])
+            nc.sync.dma_start(out=whh_raw[g], in_=whh_rows[GATES.index(g)])
 
         def load_x(q):
             nc.sync.dma_start(out=x_sb[q][:], in_=x_rows[q])
 
-        def load_h(q, js=slice(0, CHUNK)):
-            nc.sync.dma_start(out=h_sb[q][:, js, :], in_=h_rows[q][:, js, :])
+        def load_h(q):
+            nc.sync.dma_start(out=h_sb[q][:], in_=h_rows[q])
 
         def load_c(q):
             c_sb[q] = work.tile([P, CHUNK, H], BF16, name="c_sb", tag="c_sb", bufs=3)
             nc.sync.dma_start(out=c_sb[q][:], in_=c_rows[q])
 
-        def gate_cols(g):
-            return slice(GATE_BLOCK[g] * H, (GATE_BLOCK[g] + 1) * H)
+        def gate_bias_rows(g):
+            return bias_rows[:, GATES.index(g) * H : (GATES.index(g) + 1) * H]
 
         def spread_bias():
             for g in DIRECT_GATES:
                 acc = sum_bank()
-                nc.tensor.matmul(out=acc[:], lhsT=ones[:], rhs=bias_rows[:, gate_cols(g)], start=True, stop=True)
+                nc.tensor.matmul(out=acc[:], lhsT=ones[:], rhs=gate_bias_rows(g), start=True, stop=True)
                 nc.scalar.copy(out=bias_spread[g][:], in_=acc[:])
+
+        def bias_to_partitions():
             acc = sum_bank()
-            for n, g in enumerate(TURNED_GATES):
-                for block in range(4):
+            for place, g in enumerate(TURNED_GATES):
+                for block in range(BLOCKS):
+                    col = BLOCKS * place + block
                     nc.tensor.matmul(
-                        out=acc[:, 4 * n + block : 4 * n + block + 1],
-                        lhsT=bias_rows[:, gate_cols(g)][:, block * P : (block + 1) * P],
+                        out=acc[:, col : col + 1],
+                        lhsT=gate_bias_rows(g)[:, block * P : (block + 1) * P],
                         rhs=ones[:, 0:1],
                         start=True,
                         stop=True,
                     )
-            nc.scalar.copy(out=bias_cols[:].rearrange("p g b -> p (g b)"), in_=acc[:, 0 : 4 * len(TURNED_GATES)])
+            nc.scalar.copy(out=bias_cols[:].rearrange("p g b -> p (g b)"), in_=acc[:, 0 : BLOCKS * len(TURNED_GATES)])
 
         def plain_turns(acc, raw):
             view = acc[:].bitcast(BF16)
@@ -127,45 +140,43 @@ def tile_nodelstmcell_pa_t_kernel(tc, x_t, h, c, W_ih, W_hh, b_ih, b_hh, out_0, 
 
             return [lambda half=half, j=j: turn(half, j) for half in range(2) for j in range(4)]
 
-        def copy_plain(dst, acc):
-            nc.scalar.copy(out=dst[:].rearrange("p a n -> p (a n)"), in_=acc[:].bitcast(BF16))
+        def copy_plain(dst, acc, copy):
+            copy(out=dst[:].rearrange("p a n -> p (a n)"), in_=acc[:].bitcast(BF16))
 
-        def word_turns(acc, raw, pair):
+        def word_turns(acc, raw, part):
             def turn(jj, u):
-                words = raw[:, 2 * pair + jj, :].bitcast(F32)
+                words = raw[:, 2 * part + jj, :].bitcast(F32)
                 col = (2 * jj + u) * P
                 nc.tensor.transpose(acc[:, col : col + P], words[:, u : 2 * P : 2], ident_f32[:])
 
             return [lambda jj=jj, u=u: turn(jj, u) for jj in range(2) for u in range(2)]
 
-        def copy_words(grouped, acc, pair, copy):
+        def copy_words(grouped, acc, part, copy):
             copy(
-                out=grouped[:].bitcast(F32)[:, pair * H : (pair + 1) * H].rearrange("p (j r u) -> p j r u", j=2, u=2),
+                out=grouped[:].bitcast(F32)[:, part * H : (part + 1) * H].rearrange("p (j r u) -> p j r u", j=2, u=2),
                 in_=acc[:].rearrange("p (j u r) -> p j r u", j=2, u=2),
             )
 
-        def run(steps):
-            for one in steps:
-                one()
-
-        def turn_plain(dst, raw):
+        def turn_plain(dst, raw, copy):
             acc = sum_bank()
             run(plain_turns(acc, raw))
-            copy_plain(dst, acc)
+            copy_plain(dst, acc, copy)
 
-        def group_words(raw, copy):
+        def group_words(raw, products):
             grouped = words_tile()
-            for pair in range(2):
+            for part in range(2):
                 acc = sum_bank()
-                run(word_turns(acc, raw, pair))
-                copy_words(grouped, acc, pair, copy)
+                run(word_turns(acc, raw, part))
+                copy_words(grouped, acc, part, on_scalar)
+                if part == 0:
+                    run(products)
             return grouped
 
-        def prepare_wih(g):
-            turn_plain(wih_t[g], wih_raw[g])
+        def prepare_wih(g, copy):
+            turn_plain(wih_t[g], wih_raw[g], copy)
 
-        def prepare_whh(g):
-            grouped = group_words(whh_raw[g], nc.scalar.copy)
+        def prepare_whh(g, products):
+            grouped = group_words(whh_raw[g], products)
             nc.vector.quantize_mx(out=whh_codes[g][:].bitcast(E5M2X4), scales=whh_scales[g][:], in_=grouped[:])
 
         def quantize_h(q):
@@ -173,24 +184,24 @@ def tile_nodelstmcell_pa_t_kernel(tc, x_t, h, c, W_ih, W_hh, b_ih, b_hh, out_0, 
             h_scales[q] = work.tile([P, CHUNK * P], U8, name="h_scales", tag="h_scales", bufs=3, align_bytes=64)
             nc.vector.quantize_mx(out=h_codes[q][:].bitcast(E5M2X4), scales=h_scales[q][:], in_=h_words[q][:])
 
-        def prepare_h(q):
-            h_words[q] = group_words(h_sb[q], nc.vector.tensor_copy)
+        def prepare_h(q, products):
+            h_words[q] = group_words(h_sb[q], products)
             quantize_h(q)
 
         def x_tr_tile():
             return work.tile([P, 2, H], BF16, name="x_tr", tag="x_tr", bufs=2)
 
-        def input_turns(t):
+        def input_turns(t, bank, copy):
             q, j = divmod(t, CHUNK)
-            if j == 1 and q + 1 < CHUNKS:
-                acc = turn_bank()
+            if j == 2 and q + 1 < CHUNKS:
+                acc = bank()
                 x_tr[q + 1] = x_tr_tile()
-                return plain_turns(acc, x_sb[q + 1]), lambda: copy_plain(x_tr[q + 1], acc)
-            if j % 2 == 0 and q + 2 < CHUNKS:
-                acc = turn_bank()
+                return plain_turns(acc, x_sb[q + 1]), lambda: copy_plain(x_tr[q + 1], acc, copy)
+            if j < 2 and q + 2 < CHUNKS:
+                acc = bank()
                 if j == 0:
                     h_words[q + 2] = words_tile()
-                return word_turns(acc, h_sb[q + 2], j // 2), lambda: copy_words(h_words[q + 2], acc, j // 2, nc.scalar.copy)
+                return word_turns(acc, h_sb[q + 2], j), lambda: copy_words(h_words[q + 2], acc, j, copy)
             return [], lambda: None
 
         def mx_product(stationary, moving):
@@ -216,73 +227,82 @@ def tile_nodelstmcell_pa_t_kernel(tc, x_t, h, c, W_ih, W_hh, b_ih, b_hh, out_0, 
             else:
                 nc.scalar.activation(out=mx_t[q, g, block][:], in_=acc[:], func=ACT.Identity, bias=bias)
 
-        def plain_product(t, g, between, behind):
+        def plain_pass(acc, t, g, half, stop):
             q, j = divmod(t, CHUNK)
-            cols = slice(j * P, (j + 1) * P)
-            acc = sum_bank()
-            closes = g in DIRECT_GATES
-            nc.tensor.matmul(out=acc[:], lhsT=x_tr[q][:, 0, cols], rhs=wih_t[g][:, 0, :], start=True, stop=False)
-            run(between(acc))
-            nc.tensor.matmul(out=acc[:], lhsT=x_tr[q][:, 1, cols], rhs=wih_t[g][:, 1, :], start=False, stop=closes)
-            run(behind(acc))
-            return acc
+            nc.tensor.matmul(
+                out=acc[:],
+                lhsT=x_tr[q][:, half, j * P : (j + 1) * P],
+                rhs=wih_t[g][:, half, :],
+                start=half == 0,
+                stop=stop,
+            )
 
         def turned_gate(t, g, dst):
             q, j = divmod(t, CHUNK)
+            acc = sum_bank()
+            for half in range(2):
+                plain_pass(acc, t, g, half, stop=False)
+                for block in (2 * half, 2 * half + 1):
+                    nc.tensor.matmul(
+                        out=acc[:, block * P : (block + 1) * P],
+                        lhsT=mx_t[q, g, block][:, j * P : (j + 1) * P],
+                        rhs=ident_f32[:],
+                        is_transpose=True,
+                        start=False,
+                        stop=block == BLOCKS - 1,
+                    )
+            nc.scalar.activation(out=dst, in_=acc[:], func=TURNED_FUNC[g])
 
-            def add_mx(acc, block):
-                nc.tensor.matmul(
-                    out=acc[:, block * P : (block + 1) * P],
-                    lhsT=mx_t[q, g, block][:, j * P : (j + 1) * P],
-                    rhs=ident_f32[:],
-                    is_transpose=True,
-                    start=False,
-                    stop=block == 3,
-                )
+        def z_of(t, g):
+            return z_fo[t][:, DIRECT_GATES.index(g), :]
 
-            acc = plain_product(
-                t,
-                g,
-                lambda acc: [lambda: add_mx(acc, 0), lambda: add_mx(acc, 1)],
-                lambda acc: [lambda: add_mx(acc, 2), lambda: add_mx(acc, 3)],
-            )
-            nc.scalar.activation(out=dst, in_=acc[:], func=GATE_FUNC[g])
+        def direct_plain(t, g, turns):
+            acc = sum_bank()
+            for half in range(2):
+                plain_pass(acc, t, g, half, stop=half == 1)
+                run(turns[half::2])
+            nc.vector.tensor_tensor(out=z_of(t, g), in0=acc[:], in1=bias_spread[g][:], op=ALU.add)
 
-        def direct_plain(t, g, z, between, behind):
-            acc = plain_product(t, g, lambda acc: between, lambda acc: behind)
-            nc.vector.tensor_tensor(out=z, in0=acc[:], in1=bias_spread[g][:], op=ALU.add)
-
-        def direct_mx(t, g, z):
+        def direct_mx(t, g):
             q, j = divmod(t, CHUNK)
-            cols = slice(j * P, (j + 1) * P)
-            acc = mx_product((h_codes[q][:, cols], h_scales[q][:, cols]), (whh_codes[g][:], whh_scales[g][:]))
-            nc.vector.tensor_tensor(out=z, in0=acc[:], in1=z, op=ALU.add)
+            rows = slice(j * P, (j + 1) * P)
+            acc = mx_product((h_codes[q][:, rows], h_scales[q][:, rows]), (whh_codes[g][:], whh_scales[g][:]))
+            nc.vector.tensor_tensor(out=z_of(t, g), in0=acc[:], in1=z_of(t, g), op=ALU.add)
 
-        def gates_of_tile(t, prepare, scalar_meanwhile):
+        def sigmoids_fo(t):
+            s, n = divmod(t, 2)
+            nc.scalar.activation(out=s_fo[s][:, :, n, :], in_=z_fo[t][:], func=ACT.Sigmoid)
+
+        def gates_of_tile(t):
             q, j = divmod(t, CHUNK)
             s, n = divmod(t, 2)
-            turns, copy_turned = input_turns(t)
-            z = pair_tile("z_fo", 2)
+            turns, copy_turned = input_turns(t, turn_bank, on_scalar)
+            z_fo[t] = pair_tile("z_fo", 2)
             turned_gate(t, "i", s_i[s][:, n, :])
-            scalar_meanwhile()
-            prepare[0]()
-            direct_plain(t, "f", z[:, 0, :], turns[0::3], turns[1::3])
-            prepare[1]()
+            if n == 1:
+                sigmoids_fo(t - 1)
+            direct_plain(t, "f", turns)
             turned_gate(t, "g", t_g[s][:, n, :])
-            prepare[2]()
-            direct_plain(t, "o", z[:, 1, :], turns[2::3], [])
-            if q + 1 < CHUNKS:
-                mx_turned(q + 1, "g", j)
             copy_turned()
-            direct_mx(t, "f", z[:, 0, :])
-            direct_mx(t, "o", z[:, 1, :])
+            direct_plain(t, "o", [])
+            first, second = ("g", "i") if j < VECTOR_BLOCKS else ("i", "g")
             if q + 1 < CHUNKS:
-                mx_turned(q + 1, "i", j)
-            return lambda: nc.scalar.activation(out=s_fo[s][:, :, n, :], in_=z[:], func=ACT.Sigmoid)
+                mx_turned(q + 1, first, j)
+            for g in DIRECT_GATES:
+                direct_mx(t, g)
+            if q + 1 < CHUNKS:
+                mx_turned(q + 1, second, j)
+
+        both_tiles = slice(0, 2)
 
         def rows_of_pair(s):
             q, half = divmod(s, 2)
             return q, slice(2 * half, 2 * half + 2)
+
+        def gate_tiles(s):
+            s_i[s] = pair_tile("s_i", 2)
+            t_g[s] = pair_tile("t_g", 2)
+            s_fo[s] = s_fo_sized(F32, [P, 2, 2, H])
 
         def input_term(s):
             nc.vector.tensor_tensor(out=s_i[s][:], in0=s_i[s][:], in1=t_g[s][:], op=ALU.mult)
@@ -293,63 +313,56 @@ def tile_nodelstmcell_pa_t_kernel(tc, x_t, h, c, W_ih, W_hh, b_ih, b_hh, out_0, 
             if s % 2 == 0 and q >= 1 and q + 2 < CHUNKS:
                 load_c(q + 2)
 
-        def cell(s, engine, ns=slice(0, 2)):
+        def cell(s, engine, ns):
             q, js = rows_of_pair(s)
             if ns.start == 0:
                 c_new[s] = pair_tile("c_new", 3)
             engine.tensor_tensor(out=c_new[s][:, ns, :], in0=s_fo[s][:, 0, ns, :], in1=s_i[s][:, ns, :], op=ALU.add)
             nc.sync.dma_start(out=c_out[q][:, js, :][:, ns, :], in_=c_new[s][:, ns, :])
 
-        def tanh_c(s, ns=slice(0, 2)):
+        def tanh_c(s, ns):
             if ns.start == 0:
                 t_c[s] = pair_tile("t_c", 2)
             nc.scalar.activation(out=t_c[s][:, ns, :], in_=c_new[s][:, ns, :], func=ACT.Tanh)
 
-        def hidden(s, engine, ns=slice(0, 2)):
+        def hidden(s, engine, ns):
             q, js = rows_of_pair(s)
-            h_new = pair_tile("h_new", 2)
+            h_new = pair_tile("h_new", 3)
             engine.tensor_tensor(out=h_new[:, ns, :], in0=s_fo[s][:, 1, ns, :], in1=t_c[s][:, ns, :], op=ALU.mult)
             nc.sync.dma_start(out=h_out[q][:, js, :][:, ns, :], in_=h_new[:, ns, :])
 
-        nothing = [lambda: None] * 3
-
-        def step(s, prepare):
+        def step(s):
             q, half = divmod(s, 2)
-            if half == 0 and q >= 1 and q + 1 < CHUNKS:
+            if half == 0 and q + 1 < CHUNKS:
                 quantize_h(q + 1)
-            if s >= 1:
-                input_term(s - 1)
-                forget_term(s - 1)
+            input_term(s - 1)
+            forget_term(s - 1)
+            cell(s - 1, nc.gpsimd, both_tiles)
             if s >= 2:
-                tanh_c(s - 2)
-            if s >= 1:
-                cell(s - 1, nc.gpsimd)
-            if s >= 2:
-                hidden(s - 2, nc.gpsimd)
-            s_i[s] = pair_tile("s_i", 2)
-            t_g[s] = pair_tile("t_g", 2)
-            s_fo[s] = s_fo_sized(F32, [P, 2, 2, H])
-            first_sigmoids = gates_of_tile(2 * s, prepare, lambda: None)
-            gates_of_tile(2 * s + 1, nothing, first_sigmoids)()
+                tanh_c(s - 2, both_tiles)
+                hidden(s - 2, nc.gpsimd, both_tiles)
+            gate_tiles(s)
+            gates_of_tile(2 * s)
+            gates_of_tile(2 * s + 1)
+            if s == PAIRS - 1:
+                tanh_c(s - 1, both_tiles)
+            sigmoids_fo(2 * s + 1)
 
         nc.vector.memset(bias_rows[:].bitcast(I32), 0)
         nc.vector.memset(ones[:], 1.0)
         make_identity(nc, ident_f32[:])
         make_identity(nc, ident_bf[:])
-        load_h(0, slice(0, 2))
-        load_h(0, slice(2, 4))
+        load_wih("f")
+        load_x(0)
         nc.sync.dma_start(out=bias_rows[0:1, :], in_=b_ih.rearrange("(o n) -> o n", o=1))
         nc.sync.dma_start(out=bias_rows[1:2, :], in_=b_hh.rearrange("(o n) -> o n", o=1))
-        load_whh("i")
-        load_whh("g")
-        load_wih("i")
-        load_x(0)
-        load_wih("f")
-        load_wih("g")
-        load_whh("f")
         load_wih("o")
+        load_h(0)
+        for g in TURNED_GATES + DIRECT_GATES:
+            load_whh(g)
+        for g in TURNED_GATES:
+            load_wih(g)
         load_h(1)
-        load_whh("o")
         load_h(2)
         load_x(1)
         load_c(0)
@@ -362,38 +375,58 @@ def tile_nodelstmcell_pa_t_kernel(tc, x_t, h, c, W_ih, W_hh, b_ih, b_hh, out_0, 
             if q + 1 < CHUNKS:
                 load_h(q + 1)
 
-        prepare_h(0)
-        spread_bias()
-        prepare_whh("i")
-        prepare_whh("g")
+        for t in range(2):
+            z_fo[t] = pair_tile("z_fo", 2)
+        gate_tiles(0)
         x_tr[0] = x_tr_tile()
-        head_turns = [
-            lambda: prepare_wih("i"),
-            lambda: turn_plain(x_tr[0], x_sb[0]),
-            lambda: prepare_wih("f"),
-            lambda: prepare_wih("g"),
-        ]
-        for n, turn_operand in enumerate(head_turns):
-            for block in (2 * n % 4, 2 * n % 4 + 1):
-                mx_turned(0, TURNED_GATES[n // 2], block)
-            turn_operand()
 
-        def wih_o_and_h1():
-            prepare_wih("o")
-            prepare_h(1)
+        def first_direct_mx(g):
+            for t in range(2):
+                direct_mx(t, g)
 
-        step(0, [lambda: prepare_whh("f"), wih_o_and_h1, lambda: prepare_whh("o")])
+        def first_mx_turned(g, blocks):
+            for block in blocks:
+                mx_turned(0, g, block)
+
+        prepare_wih("f", on_vector)
+        turn_plain(x_tr[0], x_sb[0], on_scalar)
+        spread_bias()
+        prepare_wih("o", on_vector)
+        prepare_h(0, [lambda: direct_plain(0, "f", [])])
+        direct_plain(1, "f", [])
+        prepare_whh("i", [lambda: direct_plain(0, "o", [])])
+        direct_plain(1, "o", [])
+        bias_to_partitions()
+        prepare_whh("g", [])
+        prepare_whh("f", [lambda: first_mx_turned("i", (0, 1))])
+        first_mx_turned("i", (2, 3))
+        prepare_whh("o", [lambda: first_mx_turned("g", (0, 1))])
+        first_mx_turned("g", (2, 3))
+        prepare_wih("i", on_vector)
+        first_direct_mx("f")
+        prepare_wih("g", on_scalar)
+        prepare_h(1, [lambda: first_direct_mx("o")])
+        for t in range(2):
+            turned_gate(t, "i", s_i[0][:, t, :])
+            sigmoids_fo(t)
+            turns, copy_turned = input_turns(t, sum_bank, on_vector)
+            run(turns)
+            copy_turned()
+            turned_gate(t, "g", t_g[0][:, t, :])
+        for t in range(2):
+            for g in TURNED_GATES:
+                mx_turned(1, g, t)
+
         for s in range(1, PAIRS):
-            step(s, nothing)
+            step(s)
 
         last = PAIRS - 1
-        tanh_c(last - 1)
         input_term(last)
-        hidden(last - 1, nc.vector)
+        hidden(last - 1, nc.vector, both_tiles)
         forget_term(last)
-        halves = [slice(0, 1), slice(1, 2)]
-        for ns in halves:
+        single_tiles = [slice(0, 1), slice(1, 2)]
+        for ns in single_tiles:
             cell(last, nc.vector, ns)
             tanh_c(last, ns)
-        for ns in halves:
+        for ns in single_tiles:
             hidden(last, nc.vector, ns)

@@ -26,6 +26,7 @@ TURNED_GATES = "ig"
 DIRECT_GATES = "fo"
 TURNED_FUNC = {"i": ACT.Sigmoid, "g": ACT.Tanh}
 VECTOR_BLOCKS = 3
+WARM_MATMULS = 3
 
 
 def run(steps):
@@ -347,6 +348,14 @@ def tile_nodelstmcell_pa_t_kernel(tc, x_t, h, c, W_ih, W_hh, b_ih, b_hh, out_0, 
             if s == PAIRS - 1:
                 tanh_c(s - 1, both_tiles)
             sigmoids_fo(2 * s + 1)
+
+        warm_in = keep.tile([P, H], BF16, name="warm_in")
+        warm_out = keep.tile([P, 1], F32, name="warm_out")
+        nc.vector.memset(warm_in[:], 1.0)
+        warm_bank = turn_bank()
+        for repeat in range(WARM_MATMULS):
+            nc.tensor.matmul(out=warm_bank[:], lhsT=warm_in[:, 0:P], rhs=warm_in[:], start=True, stop=True)
+        nc.scalar.activation(out=warm_out[:], in_=warm_in[:, 0:1], func=ACT.Sigmoid)
 
         nc.vector.memset(bias_rows[:].bitcast(I32), 0)
         nc.vector.memset(ones[:], 1.0)

from contextlib import ExitStack

import concourse.mybir as mybir
from concourse.masks import make_identity

B, I, H = 4096, 256, 512
FLOPS = 2 * B * 4 * H * (I + H)

F32 = mybir.dt.float32
BF16 = mybir.dt.bfloat16
I32 = mybir.dt.int32
U32 = mybir.dt.uint32
U8 = mybir.dt.uint8
E5M2X4 = mybir.dt.float8_e5m2_x4
ACT = mybir.ActivationFunctionType
ALU = mybir.AluOpType

P = 128
CHUNK = 4
BLOCKS = H // P
TILES = B // P
PAIRS = TILES // 2
CHUNKS = TILES // CHUNK
GATES = "ifgo"
TURNED_GATES = "ig"
DIRECT_GATES = "fo"
TURNED_FUNC = {"i": ACT.Sigmoid, "g": ACT.Tanh}
VECTOR_BLOCKS = 3
WARM_MATMULS = 3


def run(steps):
    for one_step in steps:
        one_step()


def tile_nodelstmcell_pa_t_kernel(tc, x_t, h, c, W_ih, W_hh, b_ih, b_hh, out_0, out_1):
    nc = tc.nc
    x_rows = x_t.rearrange("(q p j) k -> q p j k", p=P, j=CHUNK)
    h_rows = h.rearrange("(q p j) k -> q p j k", p=P, j=CHUNK)
    c_rows = c.rearrange("(q p j) k -> q p j k", p=P, j=CHUNK)
    h_out = out_0.rearrange("(q p j) k -> q p j k", p=P, j=CHUNK)
    c_out = out_1.rearrange("(q p j) k -> q p j k", p=P, j=CHUNK)
    wih_rows = W_ih.rearrange("(g j p) k -> g p j k", p=P, j=BLOCKS)
    whh_rows = W_hh.rearrange("(g j p) k -> g p j k", p=P, j=BLOCKS)

    with ExitStack() as ctx:
        keep = ctx.enter_context(tc.tile_pool(name="keep", bufs=1))
        work = ctx.enter_context(tc.tile_pool(name="work", bufs=2))
        psum = ctx.enter_context(tc.psum_pool(name="psum", bufs=1))
        ctx.enter_context(tc.manual_schedule())
        on_scalar, on_vector = nc.scalar.copy, nc.vector.tensor_copy

        ident_bf = keep.tile([P, P], BF16, name="ident_bf")
        ident_f32 = keep.tile([P, P], F32, name="ident_f32")
        ones = keep.tile([P, P], BF16, name="ones")
        bias_rows = keep.tile([P, 4 * H], BF16, name="bias_rows")
        bias_spread = {g: keep.tile([P, H], F32, name="bias_spread_" + g) for g in DIRECT_GATES}
        bias_cols = keep.tile([P, len(TURNED_GATES), BLOCKS], F32, name="bias_cols")
        wih_t = {g: keep.tile([P, 2, H], BF16, name="wih_t_" + g) for g in GATES}
        whh_codes = {g: keep.tile([P, H], U32, name="whh_codes_" + g, align_bytes=64) for g in GATES}
        whh_scales = {g: keep.tile([P, H], U8, name="whh_scales_" + g, align_bytes=64) for g in GATES}
        x_sb = [keep.tile([P, CHUNK, I], BF16, name="x_sb%d" % q) for q in range(CHUNKS)]
        h_sb = [keep.tile([P, CHUNK, H], BF16, name="h_sb%d" % q) for q in range(CHUNKS)]

        wih_raw, whh_raw = {}, {}
        c_sb, x_tr, h_words, h_codes, h_scales = {}, {}, {}, {}, {}
        mx_t = {}
        z_fo = {}
        s_fo, s_i, t_g, c_new, t_c = {}, {}, {}, {}, {}

        def sum_bank():
            return psum.tile([P, H], F32, name="sums", tag="sums", bufs=7)

        def turn_bank():
            return psum.tile([P, H], F32, name="turn", tag="turn", bufs=1)

        def words_tile():
            return work.tile([P, 4 * H], BF16, name="words", tag="words", bufs=3, align_bytes=64)

        def mx_t_sized(dtype, shape):
            return work.tile(shape, dtype, name="mx_t", tag="mx_t", bufs=2 * BLOCKS * len(TURNED_GATES))

        def s_fo_sized(dtype, shape):
            return work.tile(shape, dtype, name="s_fo", tag="s_fo", bufs=3)

        def pair_tile(name, bufs):
            return work.tile([P, 2, H], F32, name=name, tag=name, bufs=bufs)

        for gates in (TURNED_GATES, DIRECT_GATES):
            two_gates = s_fo_sized(BF16, [P, 2, BLOCKS, H])
            for place, g in enumerate(gates):
                whh_raw[g] = two_gates[:, place, :, :]

        def load_wih(g):
            wih_raw[g] = mx_t_sized(BF16, [P, BLOCKS, I])
            nc.sync.dma_start(out=wih_raw[g][:], in_=wih_rows[GATES.index(g)])

        def load_whh(g):
            nc.sync.dma_start(out=whh_raw[g], in_=whh_rows[GATES.index(g)])

        def load_x(q):
            nc.sync.dma_start(out=x_sb[q][:], in_=x_rows[q])

        def load_h(q):
            nc.sync.dma_start(out=h_sb[q][:], in_=h_rows[q])

        def load_c(q):
            c_sb[q] = work.tile([P, CHUNK, H], BF16, name="c_sb", tag="c_sb", bufs=3)
            nc.sync.dma_start(out=c_sb[q][:], in_=c_rows[q])

        def gate_bias_rows(g):
            return bias_rows[:, GATES.index(g) * H : (GATES.index(g) + 1) * H]

        def spread_bias():
            for g in DIRECT_GATES:
                acc = sum_bank()
                nc.tensor.matmul(out=acc[:], lhsT=ones[:], rhs=gate_bias_rows(g), start=True, stop=True)
                nc.scalar.copy(out=bias_spread[g][:], in_=acc[:])

        def bias_to_partitions():
            acc = sum_bank()
            for place, g in enumerate(TURNED_GATES):
                for block in range(BLOCKS):
                    col = BLOCKS * place + block
                    nc.tensor.matmul(
                        out=acc[:, col : col + 1],
                        lhsT=gate_bias_rows(g)[:, block * P : (block + 1) * P],
                        rhs=ones[:, 0:1],
                        start=True,
                        stop=True,
                    )
            nc.scalar.copy(out=bias_cols[:].rearrange("p g b -> p (g b)"), in_=acc[:, 0 : BLOCKS * len(TURNED_GATES)])

        def plain_turns(acc, raw):
            view = acc[:].bitcast(BF16)

            def turn(half, j):
                col = half * H + j * P
                nc.tensor.transpose(view[:, col : col + P], raw[:, j, half * P : (half + 1) * P], ident_bf[:])

            return [lambda half=half, j=j: turn(half, j) for half in range(2) for j in range(4)]

        def copy_plain(dst, acc, copy):
            copy(out=dst[:].rearrange("p a n -> p (a n)"), in_=acc[:].bitcast(BF16))

        def word_turns(acc, raw, part):
            def turn(jj, u):
                words = raw[:, 2 * part + jj, :].bitcast(F32)
                col = (2 * jj + u) * P
                nc.tensor.transpose(acc[:, col : col + P], words[:, u : 2 * P : 2], ident_f32[:])

            return [lambda jj=jj, u=u: turn(jj, u) for jj in range(2) for u in range(2)]

        def copy_words(grouped, acc, part, copy):
            copy(
                out=grouped[:].bitcast(F32)[:, part * H : (part + 1) * H].rearrange("p (j r u) -> p j r u", j=2, u=2),
                in_=acc[:].rearrange("p (j u r) -> p j r u", j=2, u=2),
            )

        def turn_plain(dst, raw, copy):
            acc = sum_bank()
            run(plain_turns(acc, raw))
            copy_plain(dst, acc, copy)

        def group_words(raw, products):
            grouped = words_tile()
            for part in range(2):
                acc = sum_bank()
                run(word_turns(acc, raw, part))
                copy_words(grouped, acc, part, on_scalar)
                if part == 0:
                    run(products)
            return grouped

        def prepare_wih(g, copy):
            turn_plain(wih_t[g], wih_raw[g], copy)

        def prepare_whh(g, products):
            grouped = group_words(whh_raw[g], products)
            nc.vector.quantize_mx(out=whh_codes[g][:].bitcast(E5M2X4), scales=whh_scales[g][:], in_=grouped[:])

        def quantize_h(q):
            h_codes[q] = work.tile([P, CHUNK * P], U32, name="h_codes", tag="h_codes", bufs=3, align_bytes=64)
            h_scales[q] = work.tile([P, CHUNK * P], U8, name="h_scales", tag="h_scales", bufs=3, align_bytes=64)
            nc.vector.quantize_mx(out=h_codes[q][:].bitcast(E5M2X4), scales=h_scales[q][:], in_=h_words[q][:])

        def prepare_h(q, products):
            h_words[q] = group_words(h_sb[q], products)
            quantize_h(q)

        def x_tr_tile():
            return work.tile([P, 2, H], BF16, name="x_tr", tag="x_tr", bufs=2)

        def input_turns(t, bank, copy):
            q, j = divmod(t, CHUNK)
            if j == 2 and q + 1 < CHUNKS:
                acc = bank()
                x_tr[q + 1] = x_tr_tile()
                return plain_turns(acc, x_sb[q + 1]), lambda: copy_plain(x_tr[q + 1], acc, copy)
            if j < 2 and q + 2 < CHUNKS:
                acc = bank()
                if j == 0:
                    h_words[q + 2] = words_tile()
                return word_turns(acc, h_sb[q + 2], j), lambda: copy_words(h_words[q + 2], acc, j, copy)
            return [], lambda: None

        def mx_product(stationary, moving):
            acc = sum_bank()
            nc.tensor.matmul_mx(
                out=acc[:],
                lhsT=stationary[0].bitcast(E5M2X4),
                lhsT_scale=stationary[1],
                rhs=moving[0].bitcast(E5M2X4),
                rhs_scale=moving[1],
                start=True,
                stop=True,
            )
            return acc

        def mx_turned(q, g, block):
            cols = slice(block * P, (block + 1) * P)
            acc = mx_product((whh_codes[g][:, cols], whh_scales[g][:, cols]), (h_codes[q][:], h_scales[q][:]))
            mx_t[q, g, block] = mx_t_sized(F32, [P, CHUNK * P])
            bias = bias_cols[:, TURNED_GATES.index(g), block : block + 1]
            if g == "i" and block < VECTOR_BLOCKS:
                nc.vector.tensor_scalar(out=mx_t[q, g, block][:], in0=acc[:], scalar1=bias, scalar2=None, op0=ALU.add)
            else:
                nc.scalar.activation(out=mx_t[q, g, block][:], in_=acc[:], func=ACT.Identity, bias=bias)

        def plain_pass(acc, t, g, half, stop):
            q, j = divmod(t, CHUNK)
            nc.tensor.matmul(
                out=acc[:],
                lhsT=x_tr[q][:, half, j * P : (j + 1) * P],
                rhs=wih_t[g][:, half, :],
                start=half == 0,
                stop=stop,
            )

        def turned_gate(t, g, dst):
            q, j = divmod(t, CHUNK)
            acc = sum_bank()
            for half in range(2):
                plain_pass(acc, t, g, half, stop=False)
                for block in (2 * half, 2 * half + 1):
                    nc.tensor.matmul(
                        out=acc[:, block * P : (block + 1) * P],
                        lhsT=mx_t[q, g, block][:, j * P : (j + 1) * P],
                        rhs=ident_f32[:],
                        is_transpose=True,
                        start=False,
                        stop=block == BLOCKS - 1,
                    )
            nc.scalar.activation(out=dst, in_=acc[:], func=TURNED_FUNC[g])

        def z_of(t, g):
            return z_fo[t][:, DIRECT_GATES.index(g), :]

        def direct_plain(t, g, turns):
            acc = sum_bank()
            for half in range(2):
                plain_pass(acc, t, g, half, stop=half == 1)
                run(turns[half::2])
            nc.vector.tensor_tensor(out=z_of(t, g), in0=acc[:], in1=bias_spread[g][:], op=ALU.add)

        def direct_mx(t, g):
            q, j = divmod(t, CHUNK)
            rows = slice(j * P, (j + 1) * P)
            acc = mx_product((h_codes[q][:, rows], h_scales[q][:, rows]), (whh_codes[g][:], whh_scales[g][:]))
            nc.vector.tensor_tensor(out=z_of(t, g), in0=acc[:], in1=z_of(t, g), op=ALU.add)

        def sigmoids_fo(t):
            s, n = divmod(t, 2)
            nc.scalar.activation(out=s_fo[s][:, :, n, :], in_=z_fo[t][:], func=ACT.Sigmoid)

        def gates_of_tile(t):
            q, j = divmod(t, CHUNK)
            s, n = divmod(t, 2)
            turns, copy_turned = input_turns(t, turn_bank, on_scalar)
            z_fo[t] = pair_tile("z_fo", 2)
            turned_gate(t, "i", s_i[s][:, n, :])
            if n == 1:
                sigmoids_fo(t - 1)
            direct_plain(t, "f", turns)
            turned_gate(t, "g", t_g[s][:, n, :])
            copy_turned()
            direct_plain(t, "o", [])
            first, second = ("g", "i") if j < VECTOR_BLOCKS else ("i", "g")
            if q + 1 < CHUNKS:
                mx_turned(q + 1, first, j)
            for g in DIRECT_GATES:
                direct_mx(t, g)
            if q + 1 < CHUNKS:
                mx_turned(q + 1, second, j)

        both_tiles = slice(0, 2)

        def rows_of_pair(s):
            q, half = divmod(s, 2)
            return q, slice(2 * half, 2 * half + 2)

        def gate_tiles(s):
            s_i[s] = pair_tile("s_i", 2)
            t_g[s] = pair_tile("t_g", 2)
            s_fo[s] = s_fo_sized(F32, [P, 2, 2, H])

        def input_term(s):
            nc.vector.tensor_tensor(out=s_i[s][:], in0=s_i[s][:], in1=t_g[s][:], op=ALU.mult)

        def forget_term(s):
            q, js = rows_of_pair(s)
            nc.vector.tensor_tensor(out=s_fo[s][:, 0, :, :], in0=s_fo[s][:, 0, :, :], in1=c_sb[q][:, js, :], op=ALU.mult)
            if s % 2 == 0 and q >= 1 and q + 2 < CHUNKS:
                load_c(q + 2)

        def cell(s, engine, ns):
            q, js = rows_of_pair(s)
            if ns.start == 0:
                c_new[s] = pair_tile("c_new", 3)
            engine.tensor_tensor(out=c_new[s][:, ns, :], in0=s_fo[s][:, 0, ns, :], in1=s_i[s][:, ns, :], op=ALU.add)
            nc.sync.dma_start(out=c_out[q][:, js, :][:, ns, :], in_=c_new[s][:, ns, :])

        def tanh_c(s, ns):
            if ns.start == 0:
                t_c[s] = pair_tile("t_c", 2)
            nc.scalar.activation(out=t_c[s][:, ns, :], in_=c_new[s][:, ns, :], func=ACT.Tanh)

        def hidden(s, engine, ns):
            q, js = rows_of_pair(s)
            h_new = pair_tile("h_new", 3)
            engine.tensor_tensor(out=h_new[:, ns, :], in0=s_fo[s][:, 1, ns, :], in1=t_c[s][:, ns, :], op=ALU.mult)
            nc.sync.dma_start(out=h_out[q][:, js, :][:, ns, :], in_=h_new[:, ns, :])

        def step(s):
            q, half = divmod(s, 2)
            if half == 0 and q + 1 < CHUNKS:
                quantize_h(q + 1)
            input_term(s - 1)
            forget_term(s - 1)
            cell(s - 1, nc.gpsimd, both_tiles)
            if s >= 2:
                tanh_c(s - 2, both_tiles)
                hidden(s - 2, nc.gpsimd, both_tiles)
            gate_tiles(s)
            gates_of_tile(2 * s)
            gates_of_tile(2 * s + 1)
            if s == PAIRS - 1:
                tanh_c(s - 1, both_tiles)
            sigmoids_fo(2 * s + 1)

        warm_in = keep.tile([P, H], BF16, name="warm_in")
        warm_out = keep.tile([P, 1], F32, name="warm_out")
        nc.vector.memset(warm_in[:], 1.0)
        warm_bank = turn_bank()
        for repeat in range(WARM_MATMULS):
            nc.tensor.matmul(out=warm_bank[:], lhsT=warm_in[:, 0:P], rhs=warm_in[:], start=True, stop=True)
        nc.scalar.activation(out=warm_out[:], in_=warm_in[:, 0:1], func=ACT.Sigmoid)

        nc.vector.memset(bias_rows[:].bitcast(I32), 0)
        nc.vector.memset(ones[:], 1.0)
        make_identity(nc, ident_f32[:])
        make_identity(nc, ident_bf[:])
        load_wih("f")
        load_x(0)
        nc.sync.dma_start(out=bias_rows[0:1, :], in_=b_ih.rearrange("(o n) -> o n", o=1))
        nc.sync.dma_start(out=bias_rows[1:2, :], in_=b_hh.rearrange("(o n) -> o n", o=1))
        load_wih("o")
        load_h(0)
        for g in TURNED_GATES + DIRECT_GATES:
            load_whh(g)
        for g in TURNED_GATES:
            load_wih(g)
        load_h(1)
        load_h(2)
        load_x(1)
        load_c(0)
        load_c(1)
        load_h(3)
        load_x(2)
        load_c(2)
        for q in range(3, CHUNKS):
            load_x(q)
            if q + 1 < CHUNKS:
                load_h(q + 1)

        for t in range(2):
            z_fo[t] = pair_tile("z_fo", 2)
        gate_tiles(0)
        x_tr[0] = x_tr_tile()

        def first_direct_mx(g):
            for t in range(2):
                direct_mx(t, g)

        def first_mx_turned(g, blocks):
            for block in blocks:
                mx_turned(0, g, block)

        prepare_wih("f", on_vector)
        turn_plain(x_tr[0], x_sb[0], on_scalar)
        spread_bias()
        prepare_wih("o", on_vector)
        prepare_h(0, [lambda: direct_plain(0, "f", [])])
        direct_plain(1, "f", [])
        prepare_whh("i", [lambda: direct_plain(0, "o", [])])
        direct_plain(1, "o", [])
        bias_to_partitions()
        prepare_whh("g", [])
        prepare_whh("f", [lambda: first_mx_turned("i", (0, 1))])
        first_mx_turned("i", (2, 3))
        prepare_whh("o", [lambda: first_mx_turned("g", (0, 1))])
        first_mx_turned("g", (2, 3))
        prepare_wih("i", on_vector)
        first_direct_mx("f")
        prepare_wih("g", on_scalar)
        prepare_h(1, [lambda: first_direct_mx("o")])
        for t in range(2):
            turned_gate(t, "i", s_i[0][:, t, :])
            sigmoids_fo(t)
            turns, copy_turned = input_turns(t, sum_bank, on_vector)
            run(turns)
            copy_turned()
            turned_gate(t, "g", t_g[0][:, t, :])
        for t in range(2):
            for g in TURNED_GATES:
                mx_turned(1, g, t)

        for s in range(1, PAIRS):
            step(s)

        last = PAIRS - 1
        input_term(last)
        hidden(last - 1, nc.vector, both_tiles)
        forget_term(last)
        single_tiles = [slice(0, 1), slice(1, 2)]
        for ns in single_tiles:
            cell(last, nc.vector, ns)
            tanh_c(last, ns)
        for ns in single_tiles:
            hidden(last, nc.vector, ns)
